import numpy as np
import ml_dtypes


def mxq(x, axis, fmt="e4m3"):
    dtype, down = {"e4m3": (ml_dtypes.float8_e4m3fn, 7), "e5m2": (ml_dtypes.float8_e5m2, 14)}[fmt]
    v = np.moveaxis(np.asarray(x, np.float32).astype(ml_dtypes.bfloat16).astype(np.float64), axis, -1)
    blocks = v.reshape(v.shape[:-1] + (-1, 32))
    amax = np.abs(blocks).max(-1, keepdims=True)
    byte = np.maximum(np.where(amax > 0, np.frexp(amax)[1] - 1 + 127, 0) - down, 1)
    scale = np.exp2(byte - 127.0)
    codes = (blocks / scale).astype(np.float32).astype(dtype).astype(np.float64)
    return np.moveaxis((codes * scale).reshape(v.shape), -1, axis)


WIDE = False


def mx_kscale(k):
    if not WIDE:
        return np.ones(k)
    levels = np.array([10, -10, 5, -5, 0])
    a = np.random.permutation(np.resize(levels, k // 512 * 4)).reshape(k // 512, 4)
    idx = np.arange(k)
    return np.exp2(a[idx // 512, idx % 128 // 32])


BF16 = ml_dtypes.bfloat16


def bf(x):
    return np.asarray(x, np.float32).astype(BF16)


def f64(x):
    return np.asarray(x).astype(np.float64)


B, T, K, H, D, G = 1, 1024, 1024, 16, 128, 8


def setup_inputs():
    s = mx_kscale(K)
    q = np.random.standard_normal((B, T, H, D)) * 2.0
    k = np.random.standard_normal((B, K, H, D))
    v = np.random.standard_normal((B, K, H, D)) * 2.0
    q[..., 0] = 8.0
    k[..., 0] += (np.log(s) * np.sqrt(D) / 8.0)[None, :, None]
    v = v * (s.mean() / s)[None, :, None, None]
    return {"query": bf(q.reshape(B, T, H * D)), "key": bf(k), "value": bf(v)}


def reference(query, key, value):
    gq = f64(query).reshape(B, T // G, G, H, D)
    qh = gq.transpose(0, 3, 1, 2, 4).reshape(B, H, T, D)
    kh = f64(key).transpose(0, 2, 3, 1)
    vh = f64(value).transpose(0, 2, 1, 3)
    s = qh @ kh / np.sqrt(D)
    e = np.exp(s - s.max(-1, keepdims=True))
    o = (mxq(e, 3, "e4m3") @ mxq(vh, 2, "e4m3")) / e.sum(-1, keepdims=True)
    return o.transpose(0, 2, 1, 3).reshape(B, T, H * D)

@@ -1,0 +1,225 @@
+import math
+from contextlib import ExitStack
+
+import concourse.mybir as mybir
+from concourse.masks import make_identity
+
+BF16 = mybir.dt.bfloat16
+F32 = mybir.dt.float32
+U32 = mybir.dt.uint32
+U8 = mybir.dt.uint8
+FP8X4 = mybir.dt.float8_e4m3fn_x4
+ALU = mybir.AluOpType
+ACT = mybir.ActivationFunctionType
+AX = mybir.AxisListType
+
+P = 128
+T = 1024
+K = 1024
+H = 16
+D = 128
+NI = T // P
+NT = H * NI
+SCALE = 1.0 / math.sqrt(D)
+FLOPS = 2 * 2 * H * T * K * D
+VEC_COPY_EVERY = 5
+
+
+def tile_groupqueryattention_kernel(tc, query, key, value, out):
+    nc = tc.nc
+    q_v = query.flatten_outer_dims().rearrange("(i p) c -> p i c", p=P)
+    k_v = key.rearrange("b k h d -> (b k) (h d)").rearrange("(g p j) c -> p g j c", g=2, p=P, j=4)
+    v_v = value.rearrange("b k h d -> (b k) (h d)").rearrange("(g p j) c -> p g j c", g=2, p=P, j=4)
+    o_v = out.flatten_outer_dims().rearrange("(i p) c -> p i c", p=P)
+
+    with ExitStack() as ctx:
+        const = ctx.enter_context(tc.tile_pool(name="const", bufs=1))
+        raw = ctx.enter_context(tc.tile_pool(name="raw", bufs=1))
+        tp = ctx.enter_context(tc.tile_pool(name="tp", bufs=2))
+        work = ctx.enter_context(tc.tile_pool(name="work", bufs=3))
+        small = ctx.enter_context(tc.tile_pool(name="small", bufs=4))
+        ps_s = ctx.enter_context(tc.psum_pool(name="ps_s", bufs=4))
+        ps_t = ctx.enter_context(tc.psum_pool(name="ps_t", bufs=2))
+        ps_o = ctx.enter_context(tc.psum_pool(name="ps_o", bufs=2))
+
+        ident = const.tile([P, P], BF16, name="ident")
+        make_identity(nc, ident[:])
+
+        qraw = []
+        kraw = []
+        vraw = []
+        for hp in range(H // 2):
+            cols = slice(hp * 256, (hp + 1) * 256)
+            qr = raw.tile([P, NI, 256], BF16, name="qraw%d" % hp)
+            kr = raw.tile([P, 2, 4, 256], BF16, name="kraw%d" % hp)
+            vr = raw.tile([P, 2, 4, 256], BF16, name="vraw%d" % hp)
+            nc.sync.dma_start(out=kr[:, 0], in_=k_v[:, 0, :, cols])
+            nc.sync.dma_start(out=kr[:, 1], in_=k_v[:, 1, :, cols])
+            nc.sync.dma_start(out=qr[:], in_=q_v[:, :, cols])
+            nc.sync.dma_start(out=vr[:, 0], in_=v_v[:, 0, :, cols])
+            nc.sync.dma_start(out=vr[:, 1], in_=v_v[:, 1, :, cols])
+            qraw.append(qr)
+            kraw.append(kr)
+            vraw.append(vr)
+
+        kts = {}
+        qts = {}
+        vqs = {}
+        st = {}
+
+        def prep_k(h):
+            hc = slice((h % 2) * D, (h % 2) * D + D)
+            pk = ps_t.tile([P, 8, P], BF16, name="pk", tag="et")
+            for b in range(8):
+                nc.tensor.transpose(pk[:, b, :], kraw[h // 2][:, b // 4, b % 4, hc], ident[:])
+            kt = tp.tile([P, K], BF16, name="kt", tag="kt")
+            nc.vector.tensor_copy(out=kt[:], in_=pk[:].rearrange("p b c -> p (b c)"))
+            kts[h] = kt
+
+        def prep_q(h):
+            hc = slice((h % 2) * D, (h % 2) * D + D)
+            pq = ps_t.tile([P, 8, P], BF16, name="pq", tag="et")
+            for b in range(8):
+                nc.tensor.transpose(pq[:, b, :], qraw[h // 2][:, b, hc], ident[:])
+            qt = tp.tile([P, T], BF16, name="qt", tag="qt")
+            nc.vector.tensor_copy(out=qt[:], in_=pq[:].rearrange("p b c -> p (b c)"))
+            qts[h] = qt
+
+        def prep_v(h):
+            hc = slice((h % 2) * D, (h % 2) * D + D)
+            vg = tp.tile([P, 2, D, 4], BF16, name="vg", tag="vg", align_bytes=64)
+            nc.vector.tensor_copy(out=vg[:], in_=vraw[h // 2][:, :, :, hc].rearrange("p g j d -> p g d j"))
+            vq = tp.tile([P, 2 * D], U32, name="vq", tag="vq", align_bytes=64)
+            vs = tp.tile([P, 2 * D], U8, name="vs", tag="vs", align_bytes=64)
+            nc.vector.quantize_mx(
+                out=vq[:].bitcast(FP8X4), scales=vs[:], in_=vg[:].rearrange("p g d j -> p (g d j)")
+            )
+            vqs[h] = (vq, vs)
+
+        def stage_qk(n):
+            h, i = divmod(n, NI)
+            s = []
+            for hf in range(2):
+                sh = ps_s.tile([P, 512], F32, name="s%d" % hf, tag="s")
+                nc.tensor.matmul(
+                    sh[:],
+                    lhsT=qts[h][:, i * P : (i + 1) * P],
+                    rhs=kts[h][:, hf * 512 : (hf + 1) * 512],
+                    start=True,
+                    stop=True,
+                )
+                s.append(sh)
+            st[n] = {"s": s}
+
+        def stage_max(n):
+            mx = small.tile([P, 2], F32, name="mx", tag="mx")
+            for hf in range(2):
+                nc.vector.tensor_reduce(out=mx[:, hf : hf + 1], in_=st[n]["s"][hf][:], axis=AX.X, op=ALU.max)
+            nb = small.tile([P, 1], F32, name="nb", tag="nb")
+            nc.vector.tensor_scalar(
+                out=nb[:], in0=mx[:, 0:1], scalar1=mx[:, 1:2], scalar2=-SCALE, op0=ALU.max, op1=ALU.mult
+            )
+            st[n]["nb"] = nb
+
+        def stage_exp(n):
+            a = n % 4
+            if a == 0:
+                acc = small.tile([P, 8], F32, name="acc", tag="acc")
+                st["acc"] = acc
+            acc = st["acc"]
+            st[n]["acc"] = acc
+            e = work.tile([P, K], BF16, name="e", tag="e")
+            for hf in range(2):
+                nc.scalar.activation(
+                    out=e[:, hf * 512 : (hf + 1) * 512],
+                    in_=st[n]["s"][hf][:],
+                    func=ACT.Exp,
+                    bias=st[n]["nb"][:, 0:1],
+                    scale=SCALE,
+                    accum_out=acc[:, 2 * a + hf : 2 * a + hf + 1],
+                )
+            st[n]["e"] = e
+
+        def stage_tr(n):
+            et = ps_t.tile([P, 8, P], BF16, name="et", tag="et")
+            for b in range(8):
+                nc.tensor.transpose(et[:, b, :], st[n]["e"][:, b * P : (b + 1) * P], ident[:])
+            st[n]["et"] = et
+
+        def stage_copy(n):
+            grp = work.tile([P, 2, P, 4], BF16, name="grp", tag="grp", align_bytes=64)
+            src = st[n]["et"][:].rearrange("p (g j) t -> p g t j", g=2)
+            if n % VEC_COPY_EVERY == VEC_COPY_EVERY - 1:
+                nc.vector.tensor_copy(out=grp[:], in_=src)
+            else:
+                nc.scalar.copy(out=grp[:], in_=src)
+            st[n]["grp"] = grp
+
+        def stage_quant(n):
+            cq = work.tile([P, 2 * P], U32, name="cq", tag="cq", align_bytes=64)
+            cs = work.tile([P, 2 * P], U8, name="cs", tag="cs", align_bytes=64)
+            nc.vector.quantize_mx(
+                out=cq[:].bitcast(FP8X4), scales=cs[:], in_=st[n]["grp"][:].rearrange("p g t j -> p (g t j)")
+            )
+            st[n]["cq"] = cq
+            st[n]["cs"] = cs
+
+        def stage_pv(n):
+            h = n // NI
+            a = n % 4
+            if a == 0:
+                o_ps = ps_o.tile([P, 4, D], F32, name="o_ps", tag="o")
+                st["o"] = o_ps
+            o_ps = st["o"]
+            vq, vs = vqs[h]
+            for g in range(2):
+                nc.tensor.matmul_mx(
+                    out=o_ps[:, a, :],
+                    lhsT=st[n]["cq"][:, g * P : (g + 1) * P].bitcast(FP8X4),
+                    lhsT_scale=st[n]["cs"][:, g * P : (g + 1) * P],
+                    rhs=vq[:, g * D : (g + 1) * D].bitcast(FP8X4),
+                    rhs_scale=vs[:, g * D : (g + 1) * D],
+                    start=(g == 0),
+                    stop=(g == 1),
+                )
+            if a == 3:
+                h, i = divmod(n, NI)
+                lsum = small.tile([P, 4], F32, name="lsum", tag="lsum")
+                nc.vector.tensor_reduce(
+                    out=lsum[:], in_=st[n]["acc"][:].rearrange("p (a f) -> p a f", f=2), axis=AX.X, op=ALU.add
+                )
+                rin = small.tile([P, 4], F32, name="rin", tag="rin")
+                nc.vector.reciprocal(out=rin[:], in_=lsum[:])
+                osb = work.tile([P, 4, D], F32, name="osb", tag="osb")
+                nc.vector.tensor_tensor(
+                    out=osb[:], in0=o_ps[:], in1=rin[:].unsqueeze(2).to_broadcast([P, 4, D]), op=ALU.mult
+                )
+                nc.sync.dma_start(out=o_v[:, i - 3 : i + 1, h * D : (h + 1) * D], in_=osb[:])
+
+        prep_k(0)
+        prep_q(0)
+        stage_qk(0)
+        stage_max(0)
+        prep_v(0)
+        for n in range(NT + 2):
+            if 0 <= n - 2:
+                stage_quant(n - 2)
+                stage_pv(n - 2)
+            if n + 1 < NT:
+                stage_qk(n + 1)
+            if 0 <= n - 1 < NT:
+                stage_tr(n - 1)
+            if n < NT:
+                stage_exp(n)
+            if n + 1 < NT:
+                stage_max(n + 1)
+            if 0 <= n - 1 < NT:
+                stage_copy(n - 1)
+            h = n // NI
+            if h + 1 < H:
+                if n % NI == 1:
+                    prep_k(h + 1)
+                if n % NI == 3:
+                    prep_q(h + 1)
+                if n % NI == 5:
+                    prep_v(h + 1)

@@ -11,7 +11,6 @@ U8 = mybir.dt.uint8
 FP8X4 = mybir.dt.float8_e4m3fn_x4
 ALU = mybir.AluOpType
 ACT = mybir.ActivationFunctionType
-AX = mybir.AxisListType
 
 P = 128
 T = 1024
@@ -22,7 +21,8 @@ NI = T // P
 NT = H * NI
 SCALE = 1.0 / math.sqrt(D)
 FLOPS = 2 * 2 * H * T * K * D
-VEC_COPY_EVERY = 5
+PIN = True
+DIRECT_EVERY = 8
 
 
 def tile_groupqueryattention_kernel(tc, query, key, value, out):
@@ -36,19 +36,30 @@ def tile_groupqueryattention_kernel(tc, query, key, value, out):
         const = ctx.enter_context(tc.tile_pool(name="const", bufs=1))
         raw = ctx.enter_context(tc.tile_pool(name="raw", bufs=1))
         tp = ctx.enter_context(tc.tile_pool(name="tp", bufs=2))
+        vp = ctx.enter_context(tc.tile_pool(name="vp", bufs=3))
+        up = ctx.enter_context(tc.tile_pool(name="up", bufs=4))
         work = ctx.enter_context(tc.tile_pool(name="work", bufs=3))
-        small = ctx.enter_context(tc.tile_pool(name="small", bufs=4))
-        ps_s = ctx.enter_context(tc.psum_pool(name="ps_s", bufs=4))
+        gp = ctx.enter_context(tc.tile_pool(name="gp", bufs=5))
+        small = ctx.enter_context(tc.tile_pool(name="small", bufs=6))
+        ps_s = ctx.enter_context(tc.psum_pool(name="ps_s", bufs=3))
         ps_t = ctx.enter_context(tc.psum_pool(name="ps_t", bufs=2))
+        ps_p = ctx.enter_context(tc.psum_pool(name="ps_p", bufs=1))
         ps_o = ctx.enter_context(tc.psum_pool(name="ps_o", bufs=2))
+        if PIN:
+            ctx.enter_context(tc.manual_schedule())
 
         ident = const.tile([P, P], BF16, name="ident")
         make_identity(nc, ident[:])
+        warm = const.tile([P, 1], F32, name="warm")
+        warm2 = const.tile([P, 1], F32, name="warm2")
+        nc.vector.memset(warm[:], 0.0)
+        nc.scalar.activation(out=warm2[:], in_=warm[:], func=ACT.Exp)
 
-        qraw = []
-        kraw = []
-        vraw = []
-        for hp in range(H // 2):
+        qraw = {}
+        kraw = {}
+        vraw = {}
+
+        def load(hp):
             cols = slice(hp * 256, (hp + 1) * 256)
             qr = raw.tile([P, NI, 256], BF16, name="qraw%d" % hp)
             kr = raw.tile([P, 2, 4, 256], BF16, name="kraw%d" % hp)
@@ -58,18 +69,19 @@ def tile_groupqueryattention_kernel(tc, query, key, value, out):
             nc.sync.dma_start(out=qr[:], in_=q_v[:, :, cols])
             nc.sync.dma_start(out=vr[:, 0], in_=v_v[:, 0, :, cols])
             nc.sync.dma_start(out=vr[:, 1], in_=v_v[:, 1, :, cols])
-            qraw.append(qr)
-            kraw.append(kr)
-            vraw.append(vr)
+            qraw[hp] = qr
+            kraw[hp] = kr
+            vraw[hp] = vr
 
         kts = {}
         qts = {}
+        vgs = {}
         vqs = {}
         st = {}
 
         def prep_k(h):
             hc = slice((h % 2) * D, (h % 2) * D + D)
-            pk = ps_t.tile([P, 8, P], BF16, name="pk", tag="et")
+            pk = ps_p.tile([P, 8, P], BF16, name="pk", tag="pp")
             for b in range(8):
                 nc.tensor.transpose(pk[:, b, :], kraw[h // 2][:, b // 4, b % 4, hc], ident[:])
             kt = tp.tile([P, K], BF16, name="kt", tag="kt")
@@ -78,21 +90,31 @@ def tile_groupqueryattention_kernel(tc, query, key, value, out):
 
         def prep_q(h):
             hc = slice((h % 2) * D, (h % 2) * D + D)
-            pq = ps_t.tile([P, 8, P], BF16, name="pq", tag="et")
+            pq = ps_p.tile([P, 8, P], BF16, name="pq", tag="pp")
             for b in range(8):
                 nc.tensor.transpose(pq[:, b, :], qraw[h // 2][:, b, hc], ident[:])
             qt = tp.tile([P, T], BF16, name="qt", tag="qt")
-            nc.vector.tensor_copy(out=qt[:], in_=pq[:].rearrange("p b c -> p (b c)"))
+            nc.scalar.copy(out=qt[:], in_=pq[:].rearrange("p b c -> p (b c)"))
             qts[h] = qt
 
-        def prep_v(h):
+        def prep_v_group(h):
             hc = slice((h % 2) * D, (h % 2) * D + D)
-            vg = tp.tile([P, 2, D, 4], BF16, name="vg", tag="vg", align_bytes=64)
-            nc.vector.tensor_copy(out=vg[:], in_=vraw[h // 2][:, :, :, hc].rearrange("p g j d -> p g d j"))
-            vq = tp.tile([P, 2 * D], U32, name="vq", tag="vq", align_bytes=64)
-            vs = tp.tile([P, 2 * D], U8, name="vs", tag="vs", align_bytes=64)
+            vg = vp.tile([P, 2, D, 4], BF16, name="vg", tag="vg", align_bytes=64)
+            nc.gpsimd.tensor_scalar(
+                out=vg[:],
+                in0=vraw[h // 2][:, :, :, hc].rearrange("p g j d -> p g d j"),
+                scalar1=1.0,
+                scalar2=0.0,
+                op0=ALU.mult,
+                op1=ALU.add,
+            )
+            vgs[h] = vg
+
+        def prep_v_quant(h):
+            vq = vp.tile([P, 2 * D], U32, name="vq", tag="vq", align_bytes=64)
+            vs = vp.tile([P, 2 * D], U8, name="vs", tag="vs", align_bytes=64)
             nc.vector.quantize_mx(
-                out=vq[:].bitcast(FP8X4), scales=vs[:], in_=vg[:].rearrange("p g d j -> p (g d j)")
+                out=vq[:].bitcast(FP8X4), scales=vs[:], in_=vgs[h][:].rearrange("p g d j -> p (g d j)")
             )
             vqs[h] = (vq, vs)
 
@@ -112,32 +134,45 @@ def tile_groupqueryattention_kernel(tc, query, key, value, out):
             st[n] = {"s": s}
 
         def stage_max(n):
-            mx = small.tile([P, 2], F32, name="mx", tag="mx")
-            for hf in range(2):
-                nc.vector.tensor_reduce(out=mx[:, hf : hf + 1], in_=st[n]["s"][hf][:], axis=AX.X, op=ALU.max)
+            u = up.tile([P, K], F32, name="u", tag="u")
+            a0 = small.tile([P, 1], F32, name="a0", tag="a0")
             nb = small.tile([P, 1], F32, name="nb", tag="nb")
             nc.vector.tensor_scalar(
-                out=nb[:], in0=mx[:, 0:1], scalar1=mx[:, 1:2], scalar2=-SCALE, op0=ALU.max, op1=ALU.mult
+                out=u[:, 0:512],
+                in0=st[n]["s"][0][:],
+                scalar1=-SCALE,
+                scalar2=None,
+                op0=ALU.mult,
+                op1=ALU.min,
+                accum_out=a0[:],
             )
+            nc.vector.tensor_scalar(
+                out=u[:, 512:1024],
+                in0=st[n]["s"][1][:],
+                scalar1=-SCALE,
+                scalar2=a0[:, 0:1],
+                op0=ALU.mult,
+                op1=ALU.min,
+                accum_out=nb[:],
+            )
+            st[n]["u"] = u
             st[n]["nb"] = nb
 
         def stage_exp(n):
             a = n % 4
             if a == 0:
-                acc = small.tile([P, 8], F32, name="acc", tag="acc")
-                st["acc"] = acc
+                st["acc"] = small.tile([P, 4], F32, name="acc", tag="acc")
             acc = st["acc"]
             st[n]["acc"] = acc
             e = work.tile([P, K], BF16, name="e", tag="e")
-            for hf in range(2):
-                nc.scalar.activation(
-                    out=e[:, hf * 512 : (hf + 1) * 512],
-                    in_=st[n]["s"][hf][:],
-                    func=ACT.Exp,
-                    bias=st[n]["nb"][:, 0:1],
-                    scale=SCALE,
-                    accum_out=acc[:, 2 * a + hf : 2 * a + hf + 1],
-                )
+            nc.scalar.activation(
+                out=e[:],
+                in_=st[n]["u"][:],
+                func=ACT.Exp,
+                bias=st[n]["nb"][:, 0:1],
+                scale=-1.0,
+                accum_out=acc[:, a : a + 1],
+            )
             st[n]["e"] = e
 
         def stage_tr(n):
@@ -146,13 +181,35 @@ def tile_groupqueryattention_kernel(tc, query, key, value, out):
                 nc.tensor.transpose(et[:, b, :], st[n]["e"][:, b * P : (b + 1) * P], ident[:])
             st[n]["et"] = et
 
+        def is_direct(n):
+            return n % DIRECT_EVERY == DIRECT_EVERY - 1
+
         def stage_copy(n):
-            grp = work.tile([P, 2, P, 4], BF16, name="grp", tag="grp", align_bytes=64)
-            src = st[n]["et"][:].rearrange("p (g j) t -> p g t j", g=2)
-            if n % VEC_COPY_EVERY == VEC_COPY_EVERY - 1:
-                nc.vector.tensor_copy(out=grp[:], in_=src)
+            if is_direct(n):
+                grp = gp.tile([P, 2, P, 4], BF16, name="grp", tag="grp", align_bytes=64)
+                src = st[n]["et"][:].rearrange("p (g j) t -> p g t j", g=2)
+                if (n // DIRECT_EVERY) % 2 == 0:
+                    nc.vector.tensor_copy(out=grp[:], in_=src)
+                else:
+                    nc.scalar.copy(out=grp[:], in_=src)
+                st[n]["grp"] = grp
             else:
-                nc.scalar.copy(out=grp[:], in_=src)
+                pl = work.tile([P, 8, P], BF16, name="pl", tag="pl")
+                nc.scalar.copy(out=pl[:], in_=st[n]["et"][:])
+                st[n]["pl"] = pl
+
+        def stage_regroup(n):
+            if is_direct(n):
+                return
+            grp = gp.tile([P, 2, P, 4], BF16, name="grp", tag="grp", align_bytes=64)
+            nc.gpsimd.tensor_scalar(
+                out=grp[:],
+                in0=st[n]["pl"][:].rearrange("p (g j) t -> p g t j", g=2),
+                scalar1=1.0,
+                scalar2=0.0,
+                op0=ALU.mult,
+                op1=ALU.add,
+            )
             st[n]["grp"] = grp
 
         def stage_quant(n):
@@ -165,11 +222,10 @@ def tile_groupqueryattention_kernel(tc, query, key, value, out):
             st[n]["cs"] = cs
 
         def stage_pv(n):
-            h = n // NI
+            h, i = divmod(n, NI)
             a = n % 4
             if a == 0:
-                o_ps = ps_o.tile([P, 4, D], F32, name="o_ps", tag="o")
-                st["o"] = o_ps
+                st["o"] = ps_o.tile([P, 4, D], F32, name="o_ps", tag="o")
             o_ps = st["o"]
             vq, vs = vqs[h]
             for g in range(2):
@@ -183,43 +239,48 @@ def tile_groupqueryattention_kernel(tc, query, key, value, out):
                     stop=(g == 1),
                 )
             if a == 3:
-                h, i = divmod(n, NI)
-                lsum = small.tile([P, 4], F32, name="lsum", tag="lsum")
-                nc.vector.tensor_reduce(
-                    out=lsum[:], in_=st[n]["acc"][:].rearrange("p (a f) -> p a f", f=2), axis=AX.X, op=ALU.add
-                )
                 rin = small.tile([P, 4], F32, name="rin", tag="rin")
-                nc.vector.reciprocal(out=rin[:], in_=lsum[:])
+                nc.vector.reciprocal(out=rin[:], in_=st[n]["acc"][:])
                 osb = work.tile([P, 4, D], F32, name="osb", tag="osb")
                 nc.vector.tensor_tensor(
                     out=osb[:], in0=o_ps[:], in1=rin[:].unsqueeze(2).to_broadcast([P, 4, D]), op=ALU.mult
                 )
                 nc.sync.dma_start(out=o_v[:, i - 3 : i + 1, h * D : (h + 1) * D], in_=osb[:])
 
+        load(0)
+        load(1)
         prep_k(0)
         prep_q(0)
-        stage_qk(0)
-        stage_max(0)
-        prep_v(0)
-        for n in range(NT + 2):
-            if 0 <= n - 2:
-                stage_quant(n - 2)
-                stage_pv(n - 2)
-            if n + 1 < NT:
-                stage_qk(n + 1)
+        prep_v_group(0)
+        for n in range(-3, NT + 7):
+            if 0 <= n + 3 < NT:
+                stage_qk(n + 3)
+                stage_max(n + 3)
+            if 0 <= n < NT:
+                stage_exp(n)
             if 0 <= n - 1 < NT:
                 stage_tr(n - 1)
-            if n < NT:
-                stage_exp(n)
-            if n + 1 < NT:
-                stage_max(n + 1)
-            if 0 <= n - 1 < NT:
-                stage_copy(n - 1)
-            h = n // NI
-            if h + 1 < H:
-                if n % NI == 1:
-                    prep_k(h + 1)
-                if n % NI == 3:
-                    prep_q(h + 1)
-                if n % NI == 5:
-                    prep_v(h + 1)
+            if 0 <= n - 2 < NT:
+                stage_copy(n - 2)
+            if 0 <= n - 3 < NT:
+                stage_regroup(n - 3)
+            if 0 <= n - 5 < NT:
+                stage_quant(n - 5)
+            if 0 <= n - 6 < NT:
+                stage_pv(n - 6)
+            if n == 0:
+                prep_v_quant(0)
+            if 0 <= n < NT:
+                h = n // NI
+                r = n % NI
+                if h + 1 < H:
+                    if r == 0:
+                        prep_k(h + 1)
+                    if r == 2:
+                        prep_q(h + 1)
+                    if r == 3:
+                        prep_v_group(h + 1)
+                    if r == 5:
+                        prep_v_quant(h + 1)
+                if n % 16 == 1 and n // 16 + 2 < H // 2:
+                    load(n // 16 + 2)

@@ -40,6 +40,7 @@ def tile_groupqueryattention_kernel(tc, query, key, value, out):
         up = ctx.enter_context(tc.tile_pool(name="up", bufs=4))
         work = ctx.enter_context(tc.tile_pool(name="work", bufs=3))
         gp = ctx.enter_context(tc.tile_pool(name="gp", bufs=5))
+        cp = ctx.enter_context(tc.tile_pool(name="cp", bufs=8))
         small = ctx.enter_context(tc.tile_pool(name="small", bufs=6))
         ps_s = ctx.enter_context(tc.psum_pool(name="ps_s", bufs=3))
         ps_t = ctx.enter_context(tc.psum_pool(name="ps_t", bufs=2))
@@ -79,23 +80,53 @@ def tile_groupqueryattention_kernel(tc, query, key, value, out):
         vqs = {}
         st = {}
 
-        def prep_k(h):
-            hc = slice((h % 2) * D, (h % 2) * D + D)
-            pk = ps_p.tile([P, 8, P], BF16, name="pk", tag="pp")
-            for b in range(8):
-                nc.tensor.transpose(pk[:, b, :], kraw[h // 2][:, b // 4, b % 4, hc], ident[:])
-            kt = tp.tile([P, K], BF16, name="kt", tag="kt")
-            nc.vector.tensor_copy(out=kt[:], in_=pk[:].rearrange("p b c -> p (b c)"))
-            kts[h] = kt
+        def prep_tiles(kind, h):
+            pp = ps_p.tile([P, 8, P], BF16, name="pp", tag="pp")
+            return (kind, h, pp)
 
-        def prep_q(h):
+        def prep_transposes(job, blocks):
+            kind, h, pp = job
             hc = slice((h % 2) * D, (h % 2) * D + D)
-            pq = ps_p.tile([P, 8, P], BF16, name="pq", tag="pp")
-            for b in range(8):
-                nc.tensor.transpose(pq[:, b, :], qraw[h // 2][:, b, hc], ident[:])
-            qt = tp.tile([P, T], BF16, name="qt", tag="qt")
-            nc.scalar.copy(out=qt[:], in_=pq[:].rearrange("p b c -> p (b c)"))
-            qts[h] = qt
+            for b in blocks:
+                if kind == "k":
+                    nc.tensor.transpose(pp[:, b, :], kraw[h // 2][:, b // 4, b % 4, hc], ident[:])
+                else:
+                    nc.tensor.transpose(pp[:, b, :], qraw[h // 2][:, b, hc], ident[:])
+
+        def prep_copy(job):
+            kind, h, pp = job
+            if kind == "k":
+                kt = tp.tile([P, K], BF16, name="kt", tag="kt")
+                nc.vector.tensor_copy(out=kt[:], in_=pp[:].rearrange("p b c -> p (b c)"))
+                kts[h] = kt
+            else:
+                qt = tp.tile([P, T], BF16, name="qt", tag="qt")
+                nc.scalar.copy(out=qt[:], in_=pp[:].rearrange("p b c -> p (b c)"))
+                qts[h] = qt
+
+        def pe_round(n_mm, n_tr, job):
+            if n_mm is not None:
+                h, i = divmod(n_mm, NI)
+                st[n_mm] = {"s": []}
+            if n_tr is not None:
+                et = ps_t.tile([P, 8, P], BF16, name="et", tag="et")
+                st[n_tr]["et"] = et
+            for hf in range(2):
+                if n_mm is not None:
+                    sh = ps_s.tile([P, 512], F32, name="s%d" % hf, tag="s")
+                    nc.tensor.matmul(
+                        sh[:],
+                        lhsT=qts[h][:, i * P : (i + 1) * P],
+                        rhs=kts[h][:, hf * 512 : (hf + 1) * 512],
+                        start=True,
+                        stop=True,
+                    )
+                    st[n_mm]["s"].append(sh)
+                if n_tr is not None:
+                    for b in range(4 * hf, 4 * hf + 4):
+                        nc.tensor.transpose(et[:, b, :], st[n_tr]["e"][:, b * P : (b + 1) * P], ident[:])
+                if job is not None:
+                    prep_transposes(job, range(4 * hf, 4 * hf + 4))
 
         def prep_v_group(h):
             hc = slice((h % 2) * D, (h % 2) * D + D)
@@ -117,21 +148,6 @@ def tile_groupqueryattention_kernel(tc, query, key, value, out):
                 out=vq[:].bitcast(FP8X4), scales=vs[:], in_=vgs[h][:].rearrange("p g d j -> p (g d j)")
             )
             vqs[h] = (vq, vs)
-
-        def stage_qk(n):
-            h, i = divmod(n, NI)
-            s = []
-            for hf in range(2):
-                sh = ps_s.tile([P, 512], F32, name="s%d" % hf, tag="s")
-                nc.tensor.matmul(
-                    sh[:],
-                    lhsT=qts[h][:, i * P : (i + 1) * P],
-                    rhs=kts[h][:, hf * 512 : (hf + 1) * 512],
-                    start=True,
-                    stop=True,
-                )
-                s.append(sh)
-            st[n] = {"s": s}
 
         def stage_max(n):
             u = up.tile([P, K], F32, name="u", tag="u")
@@ -175,12 +191,6 @@ def tile_groupqueryattention_kernel(tc, query, key, value, out):
             )
             st[n]["e"] = e
 
-        def stage_tr(n):
-            et = ps_t.tile([P, 8, P], BF16, name="et", tag="et")
-            for b in range(8):
-                nc.tensor.transpose(et[:, b, :], st[n]["e"][:, b * P : (b + 1) * P], ident[:])
-            st[n]["et"] = et
-
         def is_direct(n):
             return n % DIRECT_EVERY == DIRECT_EVERY - 1
 
@@ -213,74 +223,75 @@ def tile_groupqueryattention_kernel(tc, query, key, value, out):
             st[n]["grp"] = grp
 
         def stage_quant(n):
-            cq = work.tile([P, 2 * P], U32, name="cq", tag="cq", align_bytes=64)
-            cs = work.tile([P, 2 * P], U8, name="cs", tag="cs", align_bytes=64)
+            cq = cp.tile([P, 2 * P], U32, name="cq", tag="cq", align_bytes=64)
+            cs = cp.tile([P, 2 * P], U8, name="cs", tag="cs", align_bytes=64)
             nc.vector.quantize_mx(
                 out=cq[:].bitcast(FP8X4), scales=cs[:], in_=st[n]["grp"][:].rearrange("p g t j -> p (g t j)")
             )
             st[n]["cq"] = cq
             st[n]["cs"] = cs
 
-        def stage_pv(n):
-            h, i = divmod(n, NI)
-            a = n % 4
-            if a == 0:
-                st["o"] = ps_o.tile([P, 4, D], F32, name="o_ps", tag="o")
-            o_ps = st["o"]
+        def stage_pv4(n3):
+            h, i = divmod(n3, NI)
+            o_ps = ps_o.tile([P, 4, D], F32, name="o_ps", tag="o")
             vq, vs = vqs[h]
-            for g in range(2):
-                nc.tensor.matmul_mx(
-                    out=o_ps[:, a, :],
-                    lhsT=st[n]["cq"][:, g * P : (g + 1) * P].bitcast(FP8X4),
-                    lhsT_scale=st[n]["cs"][:, g * P : (g + 1) * P],
-                    rhs=vq[:, g * D : (g + 1) * D].bitcast(FP8X4),
-                    rhs_scale=vs[:, g * D : (g + 1) * D],
-                    start=(g == 0),
-                    stop=(g == 1),
-                )
-            if a == 3:
-                rin = small.tile([P, 4], F32, name="rin", tag="rin")
-                nc.vector.reciprocal(out=rin[:], in_=st[n]["acc"][:])
-                osb = work.tile([P, 4, D], F32, name="osb", tag="osb")
-                nc.vector.tensor_tensor(
-                    out=osb[:], in0=o_ps[:], in1=rin[:].unsqueeze(2).to_broadcast([P, 4, D]), op=ALU.mult
-                )
-                nc.sync.dma_start(out=o_v[:, i - 3 : i + 1, h * D : (h + 1) * D], in_=osb[:])
+            for a in range(4):
+                n = n3 - 3 + a
+                for g in range(2):
+                    nc.tensor.matmul_mx(
+                        out=o_ps[:, a, :],
+                        lhsT=st[n]["cq"][:, g * P : (g + 1) * P].bitcast(FP8X4),
+                        lhsT_scale=st[n]["cs"][:, g * P : (g + 1) * P],
+                        rhs=vq[:, g * D : (g + 1) * D].bitcast(FP8X4),
+                        rhs_scale=vs[:, g * D : (g + 1) * D],
+                        start=(g == 0),
+                        stop=(g == 1),
+                    )
+            rin = small.tile([P, 4], F32, name="rin", tag="rin")
+            nc.vector.reciprocal(out=rin[:], in_=st[n3]["acc"][:])
+            osb = work.tile([P, 4, D], F32, name="osb", tag="osb")
+            nc.vector.tensor_tensor(
+                out=osb[:], in0=o_ps[:], in1=rin[:].unsqueeze(2).to_broadcast([P, 4, D]), op=ALU.mult
+            )
+            nc.sync.dma_start(out=o_v[:, i - 3 : i + 1, h * D : (h + 1) * D], in_=osb[:])
+
+        def in_range(n):
+            return n if 0 <= n < NT else None
 
         load(0)
         load(1)
-        prep_k(0)
-        prep_q(0)
+        for kind in ("k", "q"):
+            job0 = prep_tiles(kind, 0)
+            prep_transposes(job0, range(8))
+            prep_copy(job0)
         prep_v_group(0)
         for n in range(-3, NT + 7):
+            job = None
+            if 0 <= n < NT - NI and n % NI == 0:
+                job = prep_tiles("k", n // NI + 1)
+            if 0 <= n < NT - NI and n % NI == 2:
+                job = prep_tiles("q", n // NI + 1)
+            pe_round(in_range(n + 3), in_range(n - 1), job)
             if 0 <= n + 3 < NT:
-                stage_qk(n + 3)
                 stage_max(n + 3)
             if 0 <= n < NT:
                 stage_exp(n)
-            if 0 <= n - 1 < NT:
-                stage_tr(n - 1)
+            if job is not None:
+                prep_copy(job)
             if 0 <= n - 2 < NT:
                 stage_copy(n - 2)
             if 0 <= n - 3 < NT:
                 stage_regroup(n - 3)
             if 0 <= n - 5 < NT:
                 stage_quant(n - 5)
-            if 0 <= n - 6 < NT:
-                stage_pv(n - 6)
+            if 0 <= n - 6 < NT and (n - 6) % 4 == 3:
+                stage_pv4(n - 6)
             if n == 0:
                 prep_v_quant(0)
-            if 0 <= n < NT:
-                h = n // NI
-                r = n % NI
-                if h + 1 < H:
-                    if r == 0:
-                        prep_k(h + 1)
-                    if r == 2:
-                        prep_q(h + 1)
-                    if r == 3:
-                        prep_v_group(h + 1)
-                    if r == 5:
-                        prep_v_quant(h + 1)
-                if n % 16 == 1 and n // 16 + 2 < H // 2:
-                    load(n // 16 + 2)
+            if 0 <= n < NT - NI:
+                if n % NI == 3:
+                    prep_v_group(n // NI + 1)
+                if n % NI == 5:
+                    prep_v_quant(n // NI + 1)
+            if 0 <= n < NT and n % 16 == 1 and n // 16 + 2 < H // 2:
+                load(n // 16 + 2)

@@ -22,7 +22,7 @@ NT = H * NI
 SCALE = 1.0 / math.sqrt(D)
 FLOPS = 2 * 2 * H * T * K * D
 PIN = True
-DIRECT_EVERY = 8
+VEC_COPY_EVERY = 4
 
 
 def tile_groupqueryattention_kernel(tc, query, key, value, out):
@@ -37,14 +37,12 @@ def tile_groupqueryattention_kernel(tc, query, key, value, out):
         raw = ctx.enter_context(tc.tile_pool(name="raw", bufs=1))
         tp = ctx.enter_context(tc.tile_pool(name="tp", bufs=2))
         vp = ctx.enter_context(tc.tile_pool(name="vp", bufs=3))
-        up = ctx.enter_context(tc.tile_pool(name="up", bufs=4))
+        up = ctx.enter_context(tc.tile_pool(name="up", bufs=5))
         work = ctx.enter_context(tc.tile_pool(name="work", bufs=3))
         gp = ctx.enter_context(tc.tile_pool(name="gp", bufs=5))
-        cp = ctx.enter_context(tc.tile_pool(name="cp", bufs=8))
         small = ctx.enter_context(tc.tile_pool(name="small", bufs=6))
         ps_s = ctx.enter_context(tc.psum_pool(name="ps_s", bufs=3))
-        ps_t = ctx.enter_context(tc.psum_pool(name="ps_t", bufs=2))
-        ps_p = ctx.enter_context(tc.psum_pool(name="ps_p", bufs=1))
+        ps_t = ctx.enter_context(tc.psum_pool(name="ps_t", bufs=3))
         ps_o = ctx.enter_context(tc.psum_pool(name="ps_o", bufs=2))
         if PIN:
             ctx.enter_context(tc.manual_schedule())
@@ -80,53 +78,23 @@ def tile_groupqueryattention_kernel(tc, query, key, value, out):
         vqs = {}
         st = {}
 
-        def prep_tiles(kind, h):
-            pp = ps_p.tile([P, 8, P], BF16, name="pp", tag="pp")
-            return (kind, h, pp)
-
-        def prep_transposes(job, blocks):
-            kind, h, pp = job
+        def prep_k(h):
             hc = slice((h % 2) * D, (h % 2) * D + D)
-            for b in blocks:
-                if kind == "k":
-                    nc.tensor.transpose(pp[:, b, :], kraw[h // 2][:, b // 4, b % 4, hc], ident[:])
-                else:
-                    nc.tensor.transpose(pp[:, b, :], qraw[h // 2][:, b, hc], ident[:])
+            pk = ps_t.tile([P, 8, P], BF16, name="pk", tag="et")
+            for b in range(8):
+                nc.tensor.transpose(pk[:, b, :], kraw[h // 2][:, b // 4, b % 4, hc], ident[:])
+            kt = tp.tile([P, K], BF16, name="kt", tag="kt")
+            nc.vector.tensor_copy(out=kt[:], in_=pk[:].rearrange("p b c -> p (b c)"))
+            kts[h] = kt
 
-        def prep_copy(job):
-            kind, h, pp = job
-            if kind == "k":
-                kt = tp.tile([P, K], BF16, name="kt", tag="kt")
-                nc.vector.tensor_copy(out=kt[:], in_=pp[:].rearrange("p b c -> p (b c)"))
-                kts[h] = kt
-            else:
-                qt = tp.tile([P, T], BF16, name="qt", tag="qt")
-                nc.scalar.copy(out=qt[:], in_=pp[:].rearrange("p b c -> p (b c)"))
-                qts[h] = qt
-
-        def pe_round(n_mm, n_tr, job):
-            if n_mm is not None:
-                h, i = divmod(n_mm, NI)
-                st[n_mm] = {"s": []}
-            if n_tr is not None:
-                et = ps_t.tile([P, 8, P], BF16, name="et", tag="et")
-                st[n_tr]["et"] = et
-            for hf in range(2):
-                if n_mm is not None:
-                    sh = ps_s.tile([P, 512], F32, name="s%d" % hf, tag="s")
-                    nc.tensor.matmul(
-                        sh[:],
-                        lhsT=qts[h][:, i * P : (i + 1) * P],
-                        rhs=kts[h][:, hf * 512 : (hf + 1) * 512],
-                        start=True,
-                        stop=True,
-                    )
-                    st[n_mm]["s"].append(sh)
-                if n_tr is not None:
-                    for b in range(4 * hf, 4 * hf + 4):
-                        nc.tensor.transpose(et[:, b, :], st[n_tr]["e"][:, b * P : (b + 1) * P], ident[:])
-                if job is not None:
-                    prep_transposes(job, range(4 * hf, 4 * hf + 4))
+        def prep_q(h):
+            hc = slice((h % 2) * D, (h % 2) * D + D)
+            pq = ps_t.tile([P, 8, P], BF16, name="pq", tag="et")
+            for b in range(8):
+                nc.tensor.transpose(pq[:, b, :], qraw[h // 2][:, b, hc], ident[:])
+            qt = tp.tile([P, T], BF16, name="qt", tag="qt")
+            nc.scalar.copy(out=qt[:], in_=pq[:].rearrange("p b c -> p (b c)"))
+            qts[h] = qt
 
         def prep_v_group(h):
             hc = slice((h % 2) * D, (h % 2) * D + D)
@@ -149,10 +117,24 @@ def tile_groupqueryattention_kernel(tc, query, key, value, out):
             )
             vqs[h] = (vq, vs)
 
-        def stage_max(n):
+        def stage_qk(n):
+            h, i = divmod(n, NI)
+            s = []
+            for hf in range(2):
+                sh = ps_s.tile([P, 512], F32, name="s%d" % hf, tag="s")
+                nc.tensor.matmul(
+                    sh[:],
+                    lhsT=qts[h][:, i * P : (i + 1) * P],
+                    rhs=kts[h][:, hf * 512 : (hf + 1) * 512],
+                    start=True,
+                    stop=True,
+                )
+                s.append(sh)
+            st[n] = {"s": s}
+
+        def stage_max0(n):
             u = up.tile([P, K], F32, name="u", tag="u")
             a0 = small.tile([P, 1], F32, name="a0", tag="a0")
-            nb = small.tile([P, 1], F32, name="nb", tag="nb")
             nc.vector.tensor_scalar(
                 out=u[:, 0:512],
                 in0=st[n]["s"][0][:],
@@ -162,16 +144,20 @@ def tile_groupqueryattention_kernel(tc, query, key, value, out):
                 op1=ALU.min,
                 accum_out=a0[:],
             )
+            st[n]["u"] = u
+            st[n]["a0"] = a0
+
+        def stage_max1(n):
+            nb = small.tile([P, 1], F32, name="nb", tag="nb")
             nc.vector.tensor_scalar(
-                out=u[:, 512:1024],
+                out=st[n]["u"][:, 512:1024],
                 in0=st[n]["s"][1][:],
                 scalar1=-SCALE,
-                scalar2=a0[:, 0:1],
+                scalar2=st[n]["a0"][:, 0:1],
                 op0=ALU.mult,
                 op1=ALU.min,
                 accum_out=nb[:],
             )
-            st[n]["u"] = u
             st[n]["nb"] = nb
 
         def stage_exp(n):
@@ -191,107 +177,90 @@ def tile_groupqueryattention_kernel(tc, query, key, value, out):
             )
             st[n]["e"] = e
 
-        def is_direct(n):
-            return n % DIRECT_EVERY == DIRECT_EVERY - 1
+        def stage_tr(n):
+            et = ps_t.tile([P, 8, P], BF16, name="et", tag="et")
+            for b in range(8):
+                nc.tensor.transpose(et[:, b, :], st[n]["e"][:, b * P : (b + 1) * P], ident[:])
+            st[n]["et"] = et
 
         def stage_copy(n):
-            if is_direct(n):
-                grp = gp.tile([P, 2, P, 4], BF16, name="grp", tag="grp", align_bytes=64)
-                src = st[n]["et"][:].rearrange("p (g j) t -> p g t j", g=2)
-                if (n // DIRECT_EVERY) % 2 == 0:
-                    nc.vector.tensor_copy(out=grp[:], in_=src)
-                else:
-                    nc.scalar.copy(out=grp[:], in_=src)
-                st[n]["grp"] = grp
-            else:
-                pl = work.tile([P, 8, P], BF16, name="pl", tag="pl")
-                nc.scalar.copy(out=pl[:], in_=st[n]["et"][:])
-                st[n]["pl"] = pl
-
-        def stage_regroup(n):
-            if is_direct(n):
-                return
             grp = gp.tile([P, 2, P, 4], BF16, name="grp", tag="grp", align_bytes=64)
-            nc.gpsimd.tensor_scalar(
-                out=grp[:],
-                in0=st[n]["pl"][:].rearrange("p (g j) t -> p g t j", g=2),
-                scalar1=1.0,
-                scalar2=0.0,
-                op0=ALU.mult,
-                op1=ALU.add,
-            )
+            src = st[n]["et"][:].rearrange("p (g j) t -> p g t j", g=2)
+            if n % VEC_COPY_EVERY == VEC_COPY_EVERY - 1:
+                nc.vector.tensor_copy(out=grp[:], in_=src)
+            else:
+                nc.scalar.copy(out=grp[:], in_=src)
             st[n]["grp"] = grp
 
         def stage_quant(n):
-            cq = cp.tile([P, 2 * P], U32, name="cq", tag="cq", align_bytes=64)
-            cs = cp.tile([P, 2 * P], U8, name="cs", tag="cs", align_bytes=64)
+            cq = work.tile([P, 2 * P], U32, name="cq", tag="cq", align_bytes=64)
+            cs = work.tile([P, 2 * P], U8, name="cs", tag="cs", align_bytes=64)
             nc.vector.quantize_mx(
                 out=cq[:].bitcast(FP8X4), scales=cs[:], in_=st[n]["grp"][:].rearrange("p g t j -> p (g t j)")
             )
             st[n]["cq"] = cq
             st[n]["cs"] = cs
 
-        def stage_pv4(n3):
-            h, i = divmod(n3, NI)
-            o_ps = ps_o.tile([P, 4, D], F32, name="o_ps", tag="o")
+        def stage_pv(n):
+            h, i = divmod(n, NI)
+            a = n % 4
+            if a == 0:
+                st["o"] = ps_o.tile([P, 4, D], F32, name="o_ps", tag="o")
+            o_ps = st["o"]
             vq, vs = vqs[h]
-            for a in range(4):
-                n = n3 - 3 + a
-                for g in range(2):
-                    nc.tensor.matmul_mx(
-                        out=o_ps[:, a, :],
-                        lhsT=st[n]["cq"][:, g * P : (g + 1) * P].bitcast(FP8X4),
-                        lhsT_scale=st[n]["cs"][:, g * P : (g + 1) * P],
-                        rhs=vq[:, g * D : (g + 1) * D].bitcast(FP8X4),
-                        rhs_scale=vs[:, g * D : (g + 1) * D],
-                        start=(g == 0),
-                        stop=(g == 1),
-                    )
-            rin = small.tile([P, 4], F32, name="rin", tag="rin")
-            nc.vector.reciprocal(out=rin[:], in_=st[n3]["acc"][:])
-            osb = work.tile([P, 4, D], F32, name="osb", tag="osb")
-            nc.vector.tensor_tensor(
-                out=osb[:], in0=o_ps[:], in1=rin[:].unsqueeze(2).to_broadcast([P, 4, D]), op=ALU.mult
-            )
-            nc.sync.dma_start(out=o_v[:, i - 3 : i + 1, h * D : (h + 1) * D], in_=osb[:])
-
-        def in_range(n):
-            return n if 0 <= n < NT else None
+            for g in range(2):
+                nc.tensor.matmul_mx(
+                    out=o_ps[:, a, :],
+                    lhsT=st[n]["cq"][:, g * P : (g + 1) * P].bitcast(FP8X4),
+                    lhsT_scale=st[n]["cs"][:, g * P : (g + 1) * P],
+                    rhs=vq[:, g * D : (g + 1) * D].bitcast(FP8X4),
+                    rhs_scale=vs[:, g * D : (g + 1) * D],
+                    start=(g == 0),
+                    stop=(g == 1),
+                )
+            if a == 3:
+                rin = small.tile([P, 4], F32, name="rin", tag="rin")
+                nc.vector.reciprocal(out=rin[:], in_=st[n]["acc"][:])
+                osb = work.tile([P, 4, D], F32, name="osb", tag="osb")
+                nc.vector.tensor_tensor(
+                    out=osb[:], in0=o_ps[:], in1=rin[:].unsqueeze(2).to_broadcast([P, 4, D]), op=ALU.mult
+                )
+                nc.sync.dma_start(out=o_v[:, i - 3 : i + 1, h * D : (h + 1) * D], in_=osb[:])
 
         load(0)
         load(1)
-        for kind in ("k", "q"):
-            job0 = prep_tiles(kind, 0)
-            prep_transposes(job0, range(8))
-            prep_copy(job0)
+        prep_k(0)
+        prep_q(0)
         prep_v_group(0)
-        for n in range(-3, NT + 7):
-            job = None
-            if 0 <= n < NT - NI and n % NI == 0:
-                job = prep_tiles("k", n // NI + 1)
-            if 0 <= n < NT - NI and n % NI == 2:
-                job = prep_tiles("q", n // NI + 1)
-            pe_round(in_range(n + 3), in_range(n - 1), job)
+        for n in range(-3, NT + 6):
             if 0 <= n + 3 < NT:
-                stage_max(n + 3)
+                stage_qk(n + 3)
+                stage_max0(n + 3)
+            if 0 <= n - 4 < NT:
+                stage_quant(n - 4)
+            if 0 <= n + 3 < NT:
+                stage_max1(n + 3)
             if 0 <= n < NT:
                 stage_exp(n)
-            if job is not None:
-                prep_copy(job)
+            if 0 <= n - 1 < NT:
+                stage_tr(n - 1)
             if 0 <= n - 2 < NT:
                 stage_copy(n - 2)
-            if 0 <= n - 3 < NT:
-                stage_regroup(n - 3)
             if 0 <= n - 5 < NT:
-                stage_quant(n - 5)
-            if 0 <= n - 6 < NT and (n - 6) % 4 == 3:
-                stage_pv4(n - 6)
+                stage_pv(n - 5)
             if n == 0:
                 prep_v_quant(0)
-            if 0 <= n < NT - NI:
-                if n % NI == 3:
-                    prep_v_group(n // NI + 1)
-                if n % NI == 5:
-                    prep_v_quant(n // NI + 1)
-            if 0 <= n < NT and n % 16 == 1 and n // 16 + 2 < H // 2:
-                load(n // 16 + 2)
+            if 0 <= n < NT:
+                h = n // NI
+                r = n % NI
+                if h + 1 < H:
+                    if r == 0:
+                        prep_k(h + 1)
+                    if r == 2:
+                        prep_q(h + 1)
+                    if r == 3:
+                        prep_v_group(h + 1)
+                    if r == 5:
+                        prep_v_quant(h + 1)
+                if n % 16 == 1 and n // 16 + 2 < H // 2:
+                    load(n // 16 + 2)

@@ -42,8 +42,8 @@ def tile_groupqueryattention_kernel(tc, query, key, value, out):
         gp = ctx.enter_context(tc.tile_pool(name="gp", bufs=5))
         small = ctx.enter_context(tc.tile_pool(name="small", bufs=6))
         ps_s = ctx.enter_context(tc.psum_pool(name="ps_s", bufs=3))
-        ps_t = ctx.enter_context(tc.psum_pool(name="ps_t", bufs=3))
-        ps_o = ctx.enter_context(tc.psum_pool(name="ps_o", bufs=2))
+        ps_t = ctx.enter_context(tc.psum_pool(name="ps_t", bufs=4))
+        ps_o = ctx.enter_context(tc.psum_pool(name="ps_o", bufs=1))
         if PIN:
             ctx.enter_context(tc.manual_schedule())
 
@@ -240,14 +240,14 @@ def tile_groupqueryattention_kernel(tc, query, key, value, out):
                 stage_quant(n - 4)
             if 0 <= n + 3 < NT:
                 stage_max1(n + 3)
+            if 0 <= n - 5 < NT:
+                stage_pv(n - 5)
             if 0 <= n < NT:
                 stage_exp(n)
             if 0 <= n - 1 < NT:
                 stage_tr(n - 1)
             if 0 <= n - 2 < NT:
                 stage_copy(n - 2)
-            if 0 <= n - 5 < NT:
-                stage_pv(n - 5)
             if n == 0:
                 prep_v_quant(0)
             if 0 <= n < NT:

@@ -21,7 +21,7 @@ NI = T // P
 NT = H * NI
 SCALE = 1.0 / math.sqrt(D)
 FLOPS = 2 * 2 * H * T * K * D
-PIN = True
+PIN = False
 VEC_COPY_EVERY = 4
 
 
@@ -93,7 +93,7 @@ def tile_groupqueryattention_kernel(tc, query, key, value, out):
             for b in range(8):
                 nc.tensor.transpose(pq[:, b, :], qraw[h // 2][:, b, hc], ident[:])
             qt = tp.tile([P, T], BF16, name="qt", tag="qt")
-            nc.scalar.copy(out=qt[:], in_=pq[:].rearrange("p b c -> p (b c)"))
+            nc.vector.tensor_copy(out=qt[:], in_=pq[:].rearrange("p b c -> p (b c)"))
             qts[h] = qt
 
         def prep_v_group(h):

@@ -22,7 +22,7 @@ NT = H * NI
 SCALE = 1.0 / math.sqrt(D)
 FLOPS = 2 * 2 * H * T * K * D
 PIN = False
-VEC_COPY_EVERY = 4
+VEC_COPY_EVERY = 6
 
 
 def tile_groupqueryattention_kernel(tc, query, key, value, out):

@@ -22,6 +22,7 @@ NT = H * NI
 SCALE = 1.0 / math.sqrt(D)
 FLOPS = 2 * 2 * H * T * K * D
 PIN = False
+FB = 4
 VEC_COPY_EVERY = 6
 
 
@@ -39,7 +40,8 @@ def tile_groupqueryattention_kernel(tc, query, key, value, out):
         vp = ctx.enter_context(tc.tile_pool(name="vp", bufs=3))
         up = ctx.enter_context(tc.tile_pool(name="up", bufs=5))
         work = ctx.enter_context(tc.tile_pool(name="work", bufs=3))
-        gp = ctx.enter_context(tc.tile_pool(name="gp", bufs=5))
+        gp = ctx.enter_context(tc.tile_pool(name="gp", bufs=3))
+        cp = ctx.enter_context(tc.tile_pool(name="cp", bufs=2))
         small = ctx.enter_context(tc.tile_pool(name="small", bufs=6))
         ps_s = ctx.enter_context(tc.psum_pool(name="ps_s", bufs=3))
         ps_t = ctx.enter_context(tc.psum_pool(name="ps_t", bufs=4))
@@ -184,22 +186,27 @@ def tile_groupqueryattention_kernel(tc, query, key, value, out):
             st[n]["et"] = et
 
         def stage_copy(n):
-            grp = gp.tile([P, 2, P, 4], BF16, name="grp", tag="grp", align_bytes=64)
+            if n % FB == 0:
+                st["grp"] = gp.tile([P, FB, 2, P, 4], BF16, name="grp", tag="grp", align_bytes=64)
+            grp = st["grp"]
             src = st[n]["et"][:].rearrange("p (g j) t -> p g t j", g=2)
             if n % VEC_COPY_EVERY == VEC_COPY_EVERY - 1:
-                nc.vector.tensor_copy(out=grp[:], in_=src)
+                nc.vector.tensor_copy(out=grp[:, n % FB], in_=src)
             else:
-                nc.scalar.copy(out=grp[:], in_=src)
+                nc.scalar.copy(out=grp[:, n % FB], in_=src)
             st[n]["grp"] = grp
 
-        def stage_quant(n):
-            cq = work.tile([P, 2 * P], U32, name="cq", tag="cq", align_bytes=64)
-            cs = work.tile([P, 2 * P], U8, name="cs", tag="cs", align_bytes=64)
+        def stage_quant(n_last):
+            cq = cp.tile([P, FB * 2 * P], U32, name="cq", tag="cq", align_bytes=64)
+            cs = cp.tile([P, FB * 2 * P], U8, name="cs", tag="cs", align_bytes=64)
             nc.vector.quantize_mx(
-                out=cq[:].bitcast(FP8X4), scales=cs[:], in_=st[n]["grp"][:].rearrange("p g t j -> p (g t j)")
+                out=cq[:].bitcast(FP8X4),
+                scales=cs[:],
+                in_=st[n_last]["grp"][:].rearrange("p a g t j -> p (a g t j)"),
             )
-            st[n]["cq"] = cq
-            st[n]["cs"] = cs
+            for n in range(n_last - FB + 1, n_last + 1):
+                st[n]["cq"] = cq
+                st[n]["cs"] = cs
 
         def stage_pv(n):
             h, i = divmod(n, NI)
@@ -209,10 +216,11 @@ def tile_groupqueryattention_kernel(tc, query, key, value, out):
             o_ps = st["o"]
             vq, vs = vqs[h]
             for g in range(2):
+                c0 = ((n % FB) * 2 + g) * P
                 nc.tensor.matmul_mx(
                     out=o_ps[:, a, :],
-                    lhsT=st[n]["cq"][:, g * P : (g + 1) * P].bitcast(FP8X4),
-                    lhsT_scale=st[n]["cs"][:, g * P : (g + 1) * P],
+                    lhsT=st[n]["cq"][:, c0 : c0 + P].bitcast(FP8X4),
+                    lhsT_scale=st[n]["cs"][:, c0 : c0 + P],
                     rhs=vq[:, g * D : (g + 1) * D].bitcast(FP8X4),
                     rhs_scale=vs[:, g * D : (g + 1) * D],
                     start=(g == 0),
@@ -236,12 +244,13 @@ def tile_groupqueryattention_kernel(tc, query, key, value, out):
             if 0 <= n + 3 < NT:
                 stage_qk(n + 3)
                 stage_max0(n + 3)
-            if 0 <= n - 4 < NT:
+            if 0 <= n - 4 < NT and (n - 4) % FB == FB - 1:
                 stage_quant(n - 4)
             if 0 <= n + 3 < NT:
                 stage_max1(n + 3)
-            if 0 <= n - 5 < NT:
-                stage_pv(n - 5)
+            if 0 <= n - 5 < NT and (n - 5) % FB == FB - 1:
+                for m in range(n - 5 - FB + 1, n - 5 + 1):
+                    stage_pv(m)
             if 0 <= n < NT:
                 stage_exp(n)
             if 0 <= n - 1 < NT:

@@ -23,13 +23,12 @@ SCALE = 1.0 / math.sqrt(D)
 FLOPS = 2 * 2 * H * T * K * D
 PIN = False
 FB = 4
-VEC_COPY_EVERY = 6
 
 
 def tile_groupqueryattention_kernel(tc, query, key, value, out):
     nc = tc.nc
     q_v = query.flatten_outer_dims().rearrange("(i p) c -> p i c", p=P)
-    k_v = key.rearrange("b k h d -> (b k) (h d)").rearrange("(g p j) c -> p g j c", g=2, p=P, j=4)
+    k_v = key.rearrange("b k h d -> (b k) (h d)").rearrange("(G p u) c -> p G u c", G=4, p=P, u=2)
     v_v = value.rearrange("b k h d -> (b k) (h d)").rearrange("(g p j) c -> p g j c", g=2, p=P, j=4)
     o_v = out.flatten_outer_dims().rearrange("(i p) c -> p i c", p=P)
 
@@ -51,6 +50,8 @@ def tile_groupqueryattention_kernel(tc, query, key, value, out):
 
         ident = const.tile([P, P], BF16, name="ident")
         make_identity(nc, ident[:])
+        identf = const.tile([P, P], F32, name="identf")
+        make_identity(nc, identf[:])
         warm = const.tile([P, 1], F32, name="warm")
         warm2 = const.tile([P, 1], F32, name="warm2")
         nc.vector.memset(warm[:], 0.0)
@@ -63,10 +64,10 @@ def tile_groupqueryattention_kernel(tc, query, key, value, out):
         def load(hp):
             cols = slice(hp * 256, (hp + 1) * 256)
             qr = raw.tile([P, NI, 256], BF16, name="qraw%d" % hp)
-            kr = raw.tile([P, 2, 4, 256], BF16, name="kraw%d" % hp)
+            kr = raw.tile([P, 4, 2, 256], BF16, name="kraw%d" % hp)
             vr = raw.tile([P, 2, 4, 256], BF16, name="vraw%d" % hp)
-            nc.sync.dma_start(out=kr[:, 0], in_=k_v[:, 0, :, cols])
-            nc.sync.dma_start(out=kr[:, 1], in_=k_v[:, 1, :, cols])
+            for G in range(4):
+                nc.sync.dma_start(out=kr[:, G], in_=k_v[:, G, :, cols])
             nc.sync.dma_start(out=qr[:], in_=q_v[:, :, cols])
             nc.sync.dma_start(out=vr[:, 0], in_=v_v[:, 0, :, cols])
             nc.sync.dma_start(out=vr[:, 1], in_=v_v[:, 1, :, cols])
@@ -83,8 +84,10 @@ def tile_groupqueryattention_kernel(tc, query, key, value, out):
         def prep_k(h):
             hc = slice((h % 2) * D, (h % 2) * D + D)
             pk = ps_t.tile([P, 8, P], BF16, name="pk", tag="et")
-            for b in range(8):
-                nc.tensor.transpose(pk[:, b, :], kraw[h // 2][:, b // 4, b % 4, hc], ident[:])
+            for g in range(2):
+                for u in range(2):
+                    for hh in range(2):
+                        nc.tensor.transpose(pk[:, 4 * g + 2 * u + hh, :], kraw[h // 2][:, 2 * g + hh, u, hc], ident[:])
             kt = tp.tile([P, K], BF16, name="kt", tag="kt")
             nc.vector.tensor_copy(out=kt[:], in_=pk[:].rearrange("p b c -> p (b c)"))
             kts[h] = kt
@@ -101,14 +104,15 @@ def tile_groupqueryattention_kernel(tc, query, key, value, out):
         def prep_v_group(h):
             hc = slice((h % 2) * D, (h % 2) * D + D)
             vg = vp.tile([P, 2, D, 4], BF16, name="vg", tag="vg", align_bytes=64)
-            nc.gpsimd.tensor_scalar(
-                out=vg[:],
-                in0=vraw[h // 2][:, :, :, hc].rearrange("p g j d -> p g d j"),
-                scalar1=1.0,
-                scalar2=0.0,
-                op0=ALU.mult,
-                op1=ALU.add,
-            )
+            for g in range(2):
+                nc.gpsimd.tensor_scalar(
+                    out=vg[:, g].rearrange("p d (u e) -> p d u e", u=2),
+                    in0=vraw[h // 2][:, g, :, hc].rearrange("p (e u) d -> p d u e", e=2),
+                    scalar1=1.0,
+                    scalar2=0.0,
+                    op0=ALU.mult,
+                    op1=ALU.add,
+                )
             vgs[h] = vg
 
         def prep_v_quant(h):
@@ -180,20 +184,24 @@ def tile_groupqueryattention_kernel(tc, query, key, value, out):
             st[n]["e"] = e
 
         def stage_tr(n):
-            et = ps_t.tile([P, 8, P], BF16, name="et", tag="et")
-            for b in range(8):
-                nc.tensor.transpose(et[:, b, :], st[n]["e"][:, b * P : (b + 1) * P], ident[:])
+            et = ps_t.tile([P, 4, P], F32, name="et", tag="et")
+            ew = st[n]["e"][:].bitcast(F32)
+            for b in range(4):
+                nc.tensor.transpose(et[:, b, :], ew[:, b * P : (b + 1) * P], identf[:])
             st[n]["et"] = et
 
         def stage_copy(n):
             if n % FB == 0:
                 st["grp"] = gp.tile([P, FB, 2, P, 4], BF16, name="grp", tag="grp", align_bytes=64)
             grp = st["grp"]
-            src = st[n]["et"][:].rearrange("p (g j) t -> p g t j", g=2)
-            if n % VEC_COPY_EVERY == VEC_COPY_EVERY - 1:
-                nc.vector.tensor_copy(out=grp[:, n % FB], in_=src)
-            else:
-                nc.scalar.copy(out=grp[:, n % FB], in_=src)
+            src = st[n]["et"][:].rearrange("p (g u) t -> p g t u", g=2)
+            dst = (
+                grp[:, n % FB]
+                .rearrange("p g t j -> p (g t j)")
+                .bitcast(F32)
+                .rearrange("p (g t u) -> p g t u", g=2, u=2)
+            )
+            nc.scalar.copy(out=dst, in_=src)
             st[n]["grp"] = grp
 
         def stage_quant(n_last):

@@ -42,8 +42,8 @@ def tile_groupqueryattention_kernel(tc, query, key, value, out):
         gp = ctx.enter_context(tc.tile_pool(name="gp", bufs=3))
         cp = ctx.enter_context(tc.tile_pool(name="cp", bufs=2))
         small = ctx.enter_context(tc.tile_pool(name="small", bufs=6))
-        ps_s = ctx.enter_context(tc.psum_pool(name="ps_s", bufs=3))
-        ps_t = ctx.enter_context(tc.psum_pool(name="ps_t", bufs=4))
+        ps_s = ctx.enter_context(tc.psum_pool(name="ps_s", bufs=4))
+        ps_t = ctx.enter_context(tc.psum_pool(name="ps_t", bufs=3))
         ps_o = ctx.enter_context(tc.psum_pool(name="ps_o", bufs=1))
         if PIN:
             ctx.enter_context(tc.manual_schedule())

@@ -98,7 +98,7 @@ def tile_groupqueryattention_kernel(tc, query, key, value, out):
             for b in range(8):
                 nc.tensor.transpose(pq[:, b, :], qraw[h // 2][:, b, hc], ident[:])
             qt = tp.tile([P, T], BF16, name="qt", tag="qt")
-            nc.vector.tensor_copy(out=qt[:], in_=pq[:].rearrange("p b c -> p (b c)"))
+            nc.scalar.copy(out=qt[:], in_=pq[:].rearrange("p b c -> p (b c)"))
             qts[h] = qt
 
         def prep_v_group(h):

@@ -98,7 +98,7 @@ def tile_groupqueryattention_kernel(tc, query, key, value, out):
             for b in range(8):
                 nc.tensor.transpose(pq[:, b, :], qraw[h // 2][:, b, hc], ident[:])
             qt = tp.tile([P, T], BF16, name="qt", tag="qt")
-            nc.scalar.copy(out=qt[:], in_=pq[:].rearrange("p b c -> p (b c)"))
+            nc.scalar.copy(out=qt[:].bitcast(F32), in_=pq[:].rearrange("p b c -> p (b c)").bitcast(F32))
             qts[h] = qt
 
         def prep_v_group(h):
@@ -215,6 +215,9 @@ def tile_groupqueryattention_kernel(tc, query, key, value, out):
             for n in range(n_last - FB + 1, n_last + 1):
                 st[n]["cq"] = cq
                 st[n]["cs"] = cs
+            rin = small.tile([P, 4], F32, name="rin", tag="rin")
+            nc.vector.reciprocal(out=rin[:], in_=st[n_last]["acc"][:])
+            st[n_last]["rin"] = rin
 
         def stage_pv(n):
             h, i = divmod(n, NI)
@@ -234,26 +237,32 @@ def tile_groupqueryattention_kernel(tc, query, key, value, out):
                     start=(g == 0),
                     stop=(g == 1),
                 )
-            if a == 3:
-                rin = small.tile([P, 4], F32, name="rin", tag="rin")
-                nc.vector.reciprocal(out=rin[:], in_=st[n]["acc"][:])
-                osb = work.tile([P, 4, D], F32, name="osb", tag="osb")
-                nc.vector.tensor_tensor(
-                    out=osb[:], in0=o_ps[:], in1=rin[:].unsqueeze(2).to_broadcast([P, 4, D]), op=ALU.mult
-                )
-                nc.sync.dma_start(out=o_v[:, i - 3 : i + 1, h * D : (h + 1) * D], in_=osb[:])
+            st[n]["o"] = o_ps
+
+        def stage_out(n_last):
+            h, i = divmod(n_last, NI)
+            osb = work.tile([P, 4, D], F32, name="osb", tag="osb")
+            nc.vector.tensor_tensor(
+                out=osb[:],
+                in0=st[n_last]["o"][:],
+                in1=st[n_last]["rin"][:].unsqueeze(2).to_broadcast([P, 4, D]),
+                op=ALU.mult,
+            )
+            nc.sync.dma_start(out=o_v[:, i - 3 : i + 1, h * D : (h + 1) * D], in_=osb[:])
 
         load(0)
         load(1)
         prep_k(0)
         prep_q(0)
         prep_v_group(0)
-        for n in range(-3, NT + 6):
+        for n in range(-3, NT + 7):
             if 0 <= n + 3 < NT:
                 stage_qk(n + 3)
                 stage_max0(n + 3)
             if 0 <= n - 4 < NT and (n - 4) % FB == FB - 1:
                 stage_quant(n - 4)
+            if 0 <= n - 6 < NT and (n - 6) % FB == FB - 1:
+                stage_out(n - 6)
             if 0 <= n + 3 < NT:
                 stage_max1(n + 3)
             if 0 <= n - 5 < NT and (n - 5) % FB == FB - 1:

@@ -23,6 +23,7 @@ SCALE = 1.0 / math.sqrt(D)
 FLOPS = 2 * 2 * H * T * K * D
 PIN = False
 FB = 4
+GROUP_SIZES = [FB] * (NT // FB - 1) + [2, 1, 1]
 
 
 def tile_groupqueryattention_kernel(tc, query, key, value, out):
@@ -68,7 +69,11 @@ def tile_groupqueryattention_kernel(tc, query, key, value, out):
             vr = raw.tile([P, 2, 4, 256], BF16, name="vraw%d" % hp)
             for G in range(4):
                 nc.sync.dma_start(out=kr[:, G], in_=k_v[:, G, :, cols])
-            nc.sync.dma_start(out=qr[:], in_=q_v[:, :, cols])
+            if hp == 0:
+                nc.sync.dma_start(out=qr[:, 0:2], in_=q_v[:, 0:2, cols])
+                nc.sync.dma_start(out=qr[:, 2:NI], in_=q_v[:, 2:NI, cols])
+            else:
+                nc.sync.dma_start(out=qr[:], in_=q_v[:, :, cols])
             nc.sync.dma_start(out=vr[:, 0], in_=v_v[:, 0, :, cols])
             nc.sync.dma_start(out=vr[:, 1], in_=v_v[:, 1, :, cols])
             qraw[hp] = qr
@@ -80,6 +85,17 @@ def tile_groupqueryattention_kernel(tc, query, key, value, out):
         vgs = {}
         vqs = {}
         st = {}
+        first_of = {}
+        size_of = {}
+        n0 = 0
+        for size in GROUP_SIZES:
+            for n in range(n0, n0 + size):
+                first_of[n] = n0
+                size_of[n] = size
+            n0 += size
+
+        def is_last(n):
+            return 0 <= n < NT and n - first_of[n] == size_of[n] - 1
 
         def prep_k(h):
             hc = slice((h % 2) * D, (h % 2) * D + D)
@@ -100,6 +116,35 @@ def tile_groupqueryattention_kernel(tc, query, key, value, out):
             qt = tp.tile([P, T], BF16, name="qt", tag="qt")
             nc.scalar.copy(out=qt[:].bitcast(F32), in_=pq[:].rearrange("p b c -> p (b c)").bitcast(F32))
             qts[h] = qt
+
+        def prep_first():
+            kt = tp.tile([P, K], BF16, name="kt", tag="kt")
+            qt = tp.tile([P, T], BF16, name="qt", tag="qt")
+            kts[0] = kt
+            qts[0] = qt
+
+            def k_half(g, copy):
+                pk = ps_t.tile([P, 4, P], BF16, name="pk", tag="et")
+                for u in range(2):
+                    for hh in range(2):
+                        nc.tensor.transpose(pk[:, 2 * u + hh, :], kraw[0][:, 2 * g + hh, u, 0:D], ident[:])
+                copy(
+                    out=kt[:, g * 512 : (g + 1) * 512].bitcast(F32),
+                    in_=pk[:].rearrange("p b c -> p (b c)").bitcast(F32),
+                )
+
+            def q_part(lo, hi):
+                pq = ps_t.tile([P, hi - lo, P], BF16, name="pq", tag="et")
+                for b in range(lo, hi):
+                    nc.tensor.transpose(pq[:, b - lo, :], qraw[0][:, b, 0:D], ident[:])
+                nc.scalar.copy(
+                    out=qt[:, lo * P : hi * P].bitcast(F32), in_=pq[:].rearrange("p b c -> p (b c)").bitcast(F32)
+                )
+
+            k_half(0, nc.vector.tensor_copy)
+            q_part(0, 2)
+            k_half(1, nc.scalar.copy)
+            q_part(2, NI)
 
         def prep_v_group(h):
             hc = slice((h % 2) * D, (h % 2) * D + D)
@@ -167,9 +212,9 @@ def tile_groupqueryattention_kernel(tc, query, key, value, out):
             st[n]["nb"] = nb
 
         def stage_exp(n):
-            a = n % 4
+            a = n - first_of[n]
             if a == 0:
-                st["acc"] = small.tile([P, 4], F32, name="acc", tag="acc")
+                st["acc"] = small.tile([P, size_of[n]], F32, name="acc", tag="acc")
             acc = st["acc"]
             st[n]["acc"] = acc
             e = work.tile([P, K], BF16, name="e", tag="e")
@@ -191,12 +236,12 @@ def tile_groupqueryattention_kernel(tc, query, key, value, out):
             st[n]["et"] = et
 
         def stage_copy(n):
-            if n % FB == 0:
-                st["grp"] = gp.tile([P, FB, 2, P, 4], BF16, name="grp", tag="grp", align_bytes=64)
+            if n == first_of[n]:
+                st["grp"] = gp.tile([P, size_of[n], 2, P, 4], BF16, name="grp", tag="grp", align_bytes=64)
             grp = st["grp"]
             src = st[n]["et"][:].rearrange("p (g u) t -> p g t u", g=2)
             dst = (
-                grp[:, n % FB]
+                grp[:, n - first_of[n]]
                 .rearrange("p g t j -> p (g t j)")
                 .bitcast(F32)
                 .rearrange("p (g t u) -> p g t u", g=2, u=2)
@@ -205,29 +250,30 @@ def tile_groupqueryattention_kernel(tc, query, key, value, out):
             st[n]["grp"] = grp
 
         def stage_quant(n_last):
-            cq = cp.tile([P, FB * 2 * P], U32, name="cq", tag="cq", align_bytes=64)
-            cs = cp.tile([P, FB * 2 * P], U8, name="cs", tag="cs", align_bytes=64)
+            size = size_of[n_last]
+            cq = cp.tile([P, size * 2 * P], U32, name="cq", tag="cq", align_bytes=64)
+            cs = cp.tile([P, size * 2 * P], U8, name="cs", tag="cs", align_bytes=64)
             nc.vector.quantize_mx(
                 out=cq[:].bitcast(FP8X4),
                 scales=cs[:],
                 in_=st[n_last]["grp"][:].rearrange("p a g t j -> p (a g t j)"),
             )
-            for n in range(n_last - FB + 1, n_last + 1):
+            for n in range(first_of[n_last], n_last + 1):
                 st[n]["cq"] = cq
                 st[n]["cs"] = cs
-            rin = small.tile([P, 4], F32, name="rin", tag="rin")
+            rin = small.tile([P, size], F32, name="rin", tag="rin")
             nc.vector.reciprocal(out=rin[:], in_=st[n_last]["acc"][:])
             st[n_last]["rin"] = rin
 
         def stage_pv(n):
             h, i = divmod(n, NI)
-            a = n % 4
+            a = n - first_of[n]
             if a == 0:
-                st["o"] = ps_o.tile([P, 4, D], F32, name="o_ps", tag="o")
+                st["o"] = ps_o.tile([P, size_of[n], D], F32, name="o_ps", tag="o")
             o_ps = st["o"]
             vq, vs = vqs[h]
             for g in range(2):
-                c0 = ((n % FB) * 2 + g) * P
+                c0 = (a * 2 + g) * P
                 nc.tensor.matmul_mx(
                     out=o_ps[:, a, :],
                     lhsT=st[n]["cq"][:, c0 : c0 + P].bitcast(FP8X4),
@@ -241,32 +287,32 @@ def tile_groupqueryattention_kernel(tc, query, key, value, out):
 
         def stage_out(n_last):
             h, i = divmod(n_last, NI)
-            osb = work.tile([P, 4, D], F32, name="osb", tag="osb")
+            size = size_of[n_last]
+            osb = work.tile([P, size, D], F32, name="osb", tag="osb")
             nc.vector.tensor_tensor(
                 out=osb[:],
                 in0=st[n_last]["o"][:],
-                in1=st[n_last]["rin"][:].unsqueeze(2).to_broadcast([P, 4, D]),
+                in1=st[n_last]["rin"][:].unsqueeze(2).to_broadcast([P, size, D]),
                 op=ALU.mult,
             )
-            nc.sync.dma_start(out=o_v[:, i - 3 : i + 1, h * D : (h + 1) * D], in_=osb[:])
+            nc.sync.dma_start(out=o_v[:, i - size + 1 : i + 1, h * D : (h + 1) * D], in_=osb[:])
 
         load(0)
         load(1)
-        prep_k(0)
-        prep_q(0)
+        prep_first()
         prep_v_group(0)
         for n in range(-3, NT + 7):
             if 0 <= n + 3 < NT:
                 stage_qk(n + 3)
                 stage_max0(n + 3)
-            if 0 <= n - 4 < NT and (n - 4) % FB == FB - 1:
+            if is_last(n - 4):
                 stage_quant(n - 4)
-            if 0 <= n - 6 < NT and (n - 6) % FB == FB - 1:
+            if is_last(n - 6):
                 stage_out(n - 6)
             if 0 <= n + 3 < NT:
                 stage_max1(n + 3)
-            if 0 <= n - 5 < NT and (n - 5) % FB == FB - 1:
-                for m in range(n - 5 - FB + 1, n - 5 + 1):
+            if is_last(n - 5):
+                for m in range(first_of[n - 5], n - 5 + 1):
                     stage_pv(m)
             if 0 <= n < NT:
                 stage_exp(n)

@@ -199,16 +199,18 @@ def tile_groupqueryattention_kernel(tc, query, key, value, out):
             st[n]["a0"] = a0
 
         def stage_max1(n):
-            nb = small.tile([P, 1], F32, name="nb", tag="nb")
+            a1 = small.tile([P, 1], F32, name="a1", tag="a1")
             nc.vector.tensor_scalar(
                 out=st[n]["u"][:, 512:1024],
                 in0=st[n]["s"][1][:],
                 scalar1=-SCALE,
-                scalar2=st[n]["a0"][:, 0:1],
+                scalar2=None,
                 op0=ALU.mult,
                 op1=ALU.min,
-                accum_out=nb[:],
+                accum_out=a1[:],
             )
+            nb = small.tile([P, 1], F32, name="nb", tag="nb")
+            nc.gpsimd.tensor_scalar(out=nb[:], in0=st[n]["a0"][:], scalar1=a1[:, 0:1], scalar2=None, op0=ALU.min)
             st[n]["nb"] = nb
 
         def stage_exp(n):

@@ -38,11 +38,11 @@ def tile_groupqueryattention_kernel(tc, query, key, value, out):
         raw = ctx.enter_context(tc.tile_pool(name="raw", bufs=1))
         tp = ctx.enter_context(tc.tile_pool(name="tp", bufs=2))
         vp = ctx.enter_context(tc.tile_pool(name="vp", bufs=3))
-        up = ctx.enter_context(tc.tile_pool(name="up", bufs=5))
-        work = ctx.enter_context(tc.tile_pool(name="work", bufs=3))
+        up = ctx.enter_context(tc.tile_pool(name="up", bufs=8))
+        work = ctx.enter_context(tc.tile_pool(name="work", bufs=5))
         gp = ctx.enter_context(tc.tile_pool(name="gp", bufs=3))
-        cp = ctx.enter_context(tc.tile_pool(name="cp", bufs=2))
-        small = ctx.enter_context(tc.tile_pool(name="small", bufs=6))
+        cp = ctx.enter_context(tc.tile_pool(name="cp", bufs=3))
+        small = ctx.enter_context(tc.tile_pool(name="small", bufs=12))
         ps_s = ctx.enter_context(tc.psum_pool(name="ps_s", bufs=4))
         ps_t = ctx.enter_context(tc.psum_pool(name="ps_t", bufs=3))
         ps_o = ctx.enter_context(tc.psum_pool(name="ps_o", bufs=1))
@@ -81,6 +81,8 @@ def tile_groupqueryattention_kernel(tc, query, key, value, out):
             vraw[hp] = vr
 
         kts = {}
+        pks = {}
+        pqs = {}
         qts = {}
         vgs = {}
         vqs = {}
@@ -104,8 +106,12 @@ def tile_groupqueryattention_kernel(tc, query, key, value, out):
                 for u in range(2):
                     for hh in range(2):
                         nc.tensor.transpose(pk[:, 4 * g + 2 * u + hh, :], kraw[h // 2][:, 2 * g + hh, u, hc], ident[:])
+            pks[h] = pk
+
+        def copy_k(h):
             kt = tp.tile([P, K], BF16, name="kt", tag="kt")
-            nc.vector.tensor_copy(out=kt[:], in_=pk[:].rearrange("p b c -> p (b c)"))
+            copy = nc.scalar.copy if h % 2 else nc.vector.tensor_copy
+            copy(out=kt[:].bitcast(F32), in_=pks[h][:].rearrange("p b c -> p (b c)").bitcast(F32))
             kts[h] = kt
 
         def prep_q(h):
@@ -113,8 +119,11 @@ def tile_groupqueryattention_kernel(tc, query, key, value, out):
             pq = ps_t.tile([P, 8, P], BF16, name="pq", tag="et")
             for b in range(8):
                 nc.tensor.transpose(pq[:, b, :], qraw[h // 2][:, b, hc], ident[:])
+            pqs[h] = pq
+
+        def copy_q(h):
             qt = tp.tile([P, T], BF16, name="qt", tag="qt")
-            nc.scalar.copy(out=qt[:].bitcast(F32), in_=pq[:].rearrange("p b c -> p (b c)").bitcast(F32))
+            nc.scalar.copy(out=qt[:].bitcast(F32), in_=pqs[h][:].rearrange("p b c -> p (b c)").bitcast(F32))
             qts[h] = qt
 
         def prep_first():
@@ -328,6 +337,10 @@ def tile_groupqueryattention_kernel(tc, query, key, value, out):
                 h = n // NI
                 r = n % NI
                 if h + 1 < H:
+                    if r == 2:
+                        copy_k(h + 1)
+                    if r == 4:
+                        copy_q(h + 1)
                     if r == 0:
                         prep_k(h + 1)
                     if r == 2:

@@ -21,7 +21,7 @@ NI = T // P
 NT = H * NI
 SCALE = 1.0 / math.sqrt(D)
 FLOPS = 2 * 2 * H * T * K * D
-PIN = False
+ORDERED = {mybir.EngineType.PE, mybir.EngineType.Activation, mybir.EngineType.DVE}
 FB = 4
 GROUP_SIZES = [FB] * (NT // FB - 1) + [2, 1, 1]
 
@@ -46,8 +46,6 @@ def tile_groupqueryattention_kernel(tc, query, key, value, out):
         ps_s = ctx.enter_context(tc.psum_pool(name="ps_s", bufs=4))
         ps_t = ctx.enter_context(tc.psum_pool(name="ps_t", bufs=3))
         ps_o = ctx.enter_context(tc.psum_pool(name="ps_o", bufs=1))
-        if PIN:
-            ctx.enter_context(tc.manual_schedule())
 
         ident = const.tile([P, P], BF16, name="ident")
         make_identity(nc, ident[:])
@@ -66,18 +64,22 @@ def tile_groupqueryattention_kernel(tc, query, key, value, out):
             cols = slice(hp * 256, (hp + 1) * 256)
             qr = raw.tile([P, NI, 256], BF16, name="qraw%d" % hp)
             kr = raw.tile([P, 4, 2, 256], BF16, name="kraw%d" % hp)
-            vr = raw.tile([P, 2, 4, 256], BF16, name="vraw%d" % hp)
+            if hp == 0:
+                nc.sync.dma_start(out=qr[:, 0:4], in_=q_v[:, 0:4, cols])
             for G in range(4):
                 nc.sync.dma_start(out=kr[:, G], in_=k_v[:, G, :, cols])
             if hp == 0:
-                nc.sync.dma_start(out=qr[:, 0:2], in_=q_v[:, 0:2, cols])
-                nc.sync.dma_start(out=qr[:, 2:NI], in_=q_v[:, 2:NI, cols])
+                nc.sync.dma_start(out=qr[:, 4:NI], in_=q_v[:, 4:NI, cols])
             else:
                 nc.sync.dma_start(out=qr[:], in_=q_v[:, :, cols])
-            nc.sync.dma_start(out=vr[:, 0], in_=v_v[:, 0, :, cols])
-            nc.sync.dma_start(out=vr[:, 1], in_=v_v[:, 1, :, cols])
             qraw[hp] = qr
             kraw[hp] = kr
+
+        def load_v(hp):
+            cols = slice(hp * 256, (hp + 1) * 256)
+            vr = raw.tile([P, 2, 4, 256], BF16, name="vraw%d" % hp)
+            nc.sync.dma_start(out=vr[:, 0], in_=v_v[:, 0, :, cols])
+            nc.sync.dma_start(out=vr[:, 1], in_=v_v[:, 1, :, cols])
             vraw[hp] = vr
 
         kts = {}
@@ -150,10 +152,15 @@ def tile_groupqueryattention_kernel(tc, query, key, value, out):
                     out=qt[:, lo * P : hi * P].bitcast(F32), in_=pq[:].rearrange("p b c -> p (b c)").bitcast(F32)
                 )
 
+            q_part(0, 4)
             k_half(0, nc.vector.tensor_copy)
-            q_part(0, 2)
             k_half(1, nc.scalar.copy)
-            q_part(2, NI)
+            for n in range(4):
+                stage_qk(n)
+                stage_max0(n)
+                stage_max1(n)
+                if n == 1:
+                    q_part(4, NI)
 
         def prep_v_group(h):
             hc = slice((h % 2) * D, (h % 2) * D + D)
@@ -208,6 +215,19 @@ def tile_groupqueryattention_kernel(tc, query, key, value, out):
             st[n]["a0"] = a0
 
         def stage_max1(n):
+            nb = small.tile([P, 1], F32, name="nb", tag="nb")
+            if n < FB:
+                nc.vector.tensor_scalar(
+                    out=st[n]["u"][:, 512:1024],
+                    in0=st[n]["s"][1][:],
+                    scalar1=-SCALE,
+                    scalar2=st[n]["a0"][:, 0:1],
+                    op0=ALU.mult,
+                    op1=ALU.min,
+                    accum_out=nb[:],
+                )
+                st[n]["nb"] = nb
+                return
             a1 = small.tile([P, 1], F32, name="a1", tag="a1")
             nc.vector.tensor_scalar(
                 out=st[n]["u"][:, 512:1024],
@@ -218,7 +238,6 @@ def tile_groupqueryattention_kernel(tc, query, key, value, out):
                 op1=ALU.min,
                 accum_out=a1[:],
             )
-            nb = small.tile([P, 1], F32, name="nb", tag="nb")
             nc.gpsimd.tensor_scalar(out=nb[:], in0=st[n]["a0"][:], scalar1=a1[:, 0:1], scalar2=None, op0=ALU.min)
             st[n]["nb"] = nb
 
@@ -229,6 +248,20 @@ def tile_groupqueryattention_kernel(tc, query, key, value, out):
             acc = st["acc"]
             st[n]["acc"] = acc
             e = work.tile([P, K], BF16, name="e", tag="e")
+            st[n]["e"] = e
+            if n == NT - 1:
+                acc = small.tile([P, 2], F32, name="acc2", tag="acc2")
+                st[n]["acc"] = acc
+                for hf in range(2):
+                    nc.scalar.activation(
+                        out=e[:, hf * 512 : (hf + 1) * 512],
+                        in_=st[n]["u"][:, hf * 512 : (hf + 1) * 512],
+                        func=ACT.Exp,
+                        bias=st[n]["nb"][:, 0:1],
+                        scale=-1.0,
+                        accum_out=acc[:, hf : hf + 1],
+                    )
+                return
             nc.scalar.activation(
                 out=e[:],
                 in_=st[n]["u"][:],
@@ -237,11 +270,19 @@ def tile_groupqueryattention_kernel(tc, query, key, value, out):
                 scale=-1.0,
                 accum_out=acc[:, a : a + 1],
             )
-            st[n]["e"] = e
 
         def stage_tr(n):
-            et = ps_t.tile([P, 4, P], F32, name="et", tag="et")
             ew = st[n]["e"][:].bitcast(F32)
+            if n == NT - 1:
+                st[n]["et"] = []
+                for g in range(2):
+                    et = ps_t.tile([P, 2, P], F32, name="eth", tag="et")
+                    for u in range(2):
+                        b = 2 * g + u
+                        nc.tensor.transpose(et[:, u, :], ew[:, b * P : (b + 1) * P], identf[:])
+                    st[n]["et"].append(et)
+                return
+            et = ps_t.tile([P, 4, P], F32, name="et", tag="et")
             for b in range(4):
                 nc.tensor.transpose(et[:, b, :], ew[:, b * P : (b + 1) * P], identf[:])
             st[n]["et"] = et
@@ -250,6 +291,14 @@ def tile_groupqueryattention_kernel(tc, query, key, value, out):
             if n == first_of[n]:
                 st["grp"] = gp.tile([P, size_of[n], 2, P, 4], BF16, name="grp", tag="grp", align_bytes=64)
             grp = st["grp"]
+            if n == NT - 1:
+                st[n]["grp"] = grp
+                for g, copy in ((0, nc.vector.tensor_copy), (1, nc.scalar.copy)):
+                    copy(
+                        out=grp[:, 0, g].rearrange("p t j -> p (t j)").bitcast(F32).rearrange("p (t u) -> p t u", u=2),
+                        in_=st[n]["et"][g][:].rearrange("p u t -> p t u"),
+                    )
+                return
             src = st[n]["et"][:].rearrange("p (g u) t -> p g t u", g=2)
             dst = (
                 grp[:, n - first_of[n]]
@@ -257,18 +306,32 @@ def tile_groupqueryattention_kernel(tc, query, key, value, out):
                 .bitcast(F32)
                 .rearrange("p (g t u) -> p g t u", g=2, u=2)
             )
-            nc.scalar.copy(out=dst, in_=src)
+            copy = nc.vector.tensor_copy if n == NT - 2 else nc.scalar.copy
+            copy(out=dst, in_=src)
             st[n]["grp"] = grp
 
         def stage_quant(n_last):
             size = size_of[n_last]
             cq = cp.tile([P, size * 2 * P], U32, name="cq", tag="cq", align_bytes=64)
             cs = cp.tile([P, size * 2 * P], U8, name="cs", tag="cs", align_bytes=64)
-            nc.vector.quantize_mx(
-                out=cq[:].bitcast(FP8X4),
-                scales=cs[:],
-                in_=st[n_last]["grp"][:].rearrange("p a g t j -> p (a g t j)"),
-            )
+            if n_last == NT - 1:
+                for g in range(2):
+                    nc.vector.quantize_mx(
+                        out=cq[:, g * P : (g + 1) * P].bitcast(FP8X4),
+                        scales=cs[:, g * P : (g + 1) * P],
+                        in_=st[n_last]["grp"][:, 0, g].rearrange("p t j -> p (t j)"),
+                    )
+                acc = small.tile([P, 1], F32, name="acc1", tag="acc1")
+                nc.vector.tensor_tensor(
+                    out=acc[:], in0=st[n_last]["acc"][:, 0:1], in1=st[n_last]["acc"][:, 1:2], op=ALU.add
+                )
+                st[n_last]["acc"] = acc
+            else:
+                nc.vector.quantize_mx(
+                    out=cq[:].bitcast(FP8X4),
+                    scales=cs[:],
+                    in_=st[n_last]["grp"][:].rearrange("p a g t j -> p (a g t j)"),
+                )
             for n in range(first_of[n_last], n_last + 1):
                 st[n]["cq"] = cq
                 st[n]["cs"] = cs
@@ -280,7 +343,10 @@ def tile_groupqueryattention_kernel(tc, query, key, value, out):
             h, i = divmod(n, NI)
             a = n - first_of[n]
             if a == 0:
-                st["o"] = ps_o.tile([P, size_of[n], D], F32, name="o_ps", tag="o")
+                if size_of[n] == FB:
+                    st["o"] = ps_o.tile([P, FB, D], F32, name="o_ps", tag="o")
+                else:
+                    st["o"] = ps_s.tile([P, size_of[n], D], F32, name="o_s", tag="s")
             o_ps = st["o"]
             vq, vs = vqs[h]
             for g in range(2):
@@ -308,19 +374,15 @@ def tile_groupqueryattention_kernel(tc, query, key, value, out):
             )
             nc.sync.dma_start(out=o_v[:, i - size + 1 : i + 1, h * D : (h + 1) * D], in_=osb[:])
 
-        load(0)
-        load(1)
-        prep_first()
-        prep_v_group(0)
-        for n in range(-3, NT + 7):
-            if 0 <= n + 3 < NT:
+        def step(n):
+            if 4 <= n + 3 < NT:
                 stage_qk(n + 3)
                 stage_max0(n + 3)
             if is_last(n - 4):
                 stage_quant(n - 4)
             if is_last(n - 6):
                 stage_out(n - 6)
-            if 0 <= n + 3 < NT:
+            if 4 <= n + 3 < NT:
                 stage_max1(n + 3)
             if is_last(n - 5):
                 for m in range(first_of[n - 5], n - 5 + 1):
@@ -332,6 +394,8 @@ def tile_groupqueryattention_kernel(tc, query, key, value, out):
             if 0 <= n - 2 < NT:
                 stage_copy(n - 2)
             if n == 0:
+                prep_v_group(0)
+            if n == 2:
                 prep_v_quant(0)
             if 0 <= n < NT:
                 h = n // NI
@@ -351,3 +415,15 @@ def tile_groupqueryattention_kernel(tc, query, key, value, out):
                         prep_v_quant(h + 1)
                 if n % 16 == 1 and n // 16 + 2 < H // 2:
                     load(n // 16 + 2)
+                    load_v(n // 16 + 2)
+
+        load(0)
+        load(1)
+        load_v(0)
+        load_v(1)
+        with tc.manual_schedule(engines=ORDERED):
+            prep_first()
+            for n in range(-3, FB):
+                step(n)
+        for n in range(FB, NT + 7):
+            step(n)

import math
from contextlib import ExitStack

import concourse.mybir as mybir
from concourse.masks import make_identity

BF16 = mybir.dt.bfloat16
F32 = mybir.dt.float32
U32 = mybir.dt.uint32
U8 = mybir.dt.uint8
FP8X4 = mybir.dt.float8_e4m3fn_x4
ALU = mybir.AluOpType
ACT = mybir.ActivationFunctionType

P = 128
T = 1024
K = 1024
H = 16
D = 128
NI = T // P
NT = H * NI
SCALE = 1.0 / math.sqrt(D)
FLOPS = 2 * 2 * H * T * K * D
ORDERED = {mybir.EngineType.PE, mybir.EngineType.Activation, mybir.EngineType.DVE}
FB = 4
GROUP_SIZES = [FB] * (NT // FB - 1) + [2, 1, 1]


def tile_groupqueryattention_kernel(tc, query, key, value, out):
    nc = tc.nc
    q_v = query.flatten_outer_dims().rearrange("(i p) c -> p i c", p=P)
    k_v = key.rearrange("b k h d -> (b k) (h d)").rearrange("(G p u) c -> p G u c", G=4, p=P, u=2)
    v_v = value.rearrange("b k h d -> (b k) (h d)").rearrange("(g p j) c -> p g j c", g=2, p=P, j=4)
    o_v = out.flatten_outer_dims().rearrange("(i p) c -> p i c", p=P)

    with ExitStack() as ctx:
        const = ctx.enter_context(tc.tile_pool(name="const", bufs=1))
        raw = ctx.enter_context(tc.tile_pool(name="raw", bufs=1))
        tp = ctx.enter_context(tc.tile_pool(name="tp", bufs=2))
        vp = ctx.enter_context(tc.tile_pool(name="vp", bufs=3))
        up = ctx.enter_context(tc.tile_pool(name="up", bufs=8))
        work = ctx.enter_context(tc.tile_pool(name="work", bufs=5))
        gp = ctx.enter_context(tc.tile_pool(name="gp", bufs=3))
        cp = ctx.enter_context(tc.tile_pool(name="cp", bufs=3))
        small = ctx.enter_context(tc.tile_pool(name="small", bufs=12))
        ps_s = ctx.enter_context(tc.psum_pool(name="ps_s", bufs=4))
        ps_t = ctx.enter_context(tc.psum_pool(name="ps_t", bufs=3))
        ps_o = ctx.enter_context(tc.psum_pool(name="ps_o", bufs=1))

        ident = const.tile([P, P], BF16, name="ident")
        make_identity(nc, ident[:])
        identf = const.tile([P, P], F32, name="identf")
        make_identity(nc, identf[:])
        warm = const.tile([P, 1], F32, name="warm")
        warm2 = const.tile([P, 1], F32, name="warm2")
        nc.vector.memset(warm[:], 0.0)
        nc.scalar.activation(out=warm2[:], in_=warm[:], func=ACT.Exp)

        qraw = {}
        kraw = {}
        vraw = {}

        def load(hp):
            cols = slice(hp * 256, (hp + 1) * 256)
            qr = raw.tile([P, NI, 256], BF16, name="qraw%d" % hp)
            kr = raw.tile([P, 4, 2, 256], BF16, name="kraw%d" % hp)
            if hp == 0:
                nc.sync.dma_start(out=qr[:, 0:4], in_=q_v[:, 0:4, cols])
            for G in range(4):
                nc.sync.dma_start(out=kr[:, G], in_=k_v[:, G, :, cols])
            if hp == 0:
                nc.sync.dma_start(out=qr[:, 4:NI], in_=q_v[:, 4:NI, cols])
            else:
                nc.sync.dma_start(out=qr[:], in_=q_v[:, :, cols])
            qraw[hp] = qr
            kraw[hp] = kr

        def load_v(hp):
            cols = slice(hp * 256, (hp + 1) * 256)
            vr = raw.tile([P, 2, 4, 256], BF16, name="vraw%d" % hp)
            nc.sync.dma_start(out=vr[:, 0], in_=v_v[:, 0, :, cols])
            nc.sync.dma_start(out=vr[:, 1], in_=v_v[:, 1, :, cols])
            vraw[hp] = vr

        kts = {}
        pks = {}
        pqs = {}
        qts = {}
        vgs = {}
        vqs = {}
        st = {}
        first_of = {}
        size_of = {}
        n0 = 0
        for size in GROUP_SIZES:
            for n in range(n0, n0 + size):
                first_of[n] = n0
                size_of[n] = size
            n0 += size

        def is_last(n):
            return 0 <= n < NT and n - first_of[n] == size_of[n] - 1

        def prep_k(h):
            hc = slice((h % 2) * D, (h % 2) * D + D)
            pk = ps_t.tile([P, 8, P], BF16, name="pk", tag="et")
            for g in range(2):
                for u in range(2):
                    for hh in range(2):
                        nc.tensor.transpose(pk[:, 4 * g + 2 * u + hh, :], kraw[h // 2][:, 2 * g + hh, u, hc], ident[:])
            pks[h] = pk

        def copy_k(h):
            kt = tp.tile([P, K], BF16, name="kt", tag="kt")
            copy = nc.scalar.copy if h % 2 else nc.vector.tensor_copy
            copy(out=kt[:].bitcast(F32), in_=pks[h][:].rearrange("p b c -> p (b c)").bitcast(F32))
            kts[h] = kt

        def prep_q(h):
            hc = slice((h % 2) * D, (h % 2) * D + D)
            pq = ps_t.tile([P, 8, P], BF16, name="pq", tag="et")
            for b in range(8):
                nc.tensor.transpose(pq[:, b, :], qraw[h // 2][:, b, hc], ident[:])
            pqs[h] = pq

        def copy_q(h):
            qt = tp.tile([P, T], BF16, name="qt", tag="qt")
            nc.scalar.copy(out=qt[:].bitcast(F32), in_=pqs[h][:].rearrange("p b c -> p (b c)").bitcast(F32))
            qts[h] = qt

        def prep_first():
            kt = tp.tile([P, K], BF16, name="kt", tag="kt")
            qt = tp.tile([P, T], BF16, name="qt", tag="qt")
            kts[0] = kt
            qts[0] = qt

            def k_half(g, copy):
                pk = ps_t.tile([P, 4, P], BF16, name="pk", tag="et")
                for u in range(2):
                    for hh in range(2):
                        nc.tensor.transpose(pk[:, 2 * u + hh, :], kraw[0][:, 2 * g + hh, u, 0:D], ident[:])
                copy(
                    out=kt[:, g * 512 : (g + 1) * 512].bitcast(F32),
                    in_=pk[:].rearrange("p b c -> p (b c)").bitcast(F32),
                )

            def q_part(lo, hi):
                pq = ps_t.tile([P, hi - lo, P], BF16, name="pq", tag="et")
                for b in range(lo, hi):
                    nc.tensor.transpose(pq[:, b - lo, :], qraw[0][:, b, 0:D], ident[:])
                nc.scalar.copy(
                    out=qt[:, lo * P : hi * P].bitcast(F32), in_=pq[:].rearrange("p b c -> p (b c)").bitcast(F32)
                )

            q_part(0, 4)
            k_half(0, nc.vector.tensor_copy)
            k_half(1, nc.scalar.copy)
            for n in range(4):
                stage_qk(n)
                stage_max0(n)
                stage_max1(n)
                if n == 1:
                    q_part(4, NI)

        def prep_v_group(h):
            hc = slice((h % 2) * D, (h % 2) * D + D)
            vg = vp.tile([P, 2, D, 4], BF16, name="vg", tag="vg", align_bytes=64)
            for g in range(2):
                nc.gpsimd.tensor_scalar(
                    out=vg[:, g].rearrange("p d (u e) -> p d u e", u=2),
                    in0=vraw[h // 2][:, g, :, hc].rearrange("p (e u) d -> p d u e", e=2),
                    scalar1=1.0,
                    scalar2=0.0,
                    op0=ALU.mult,
                    op1=ALU.add,
                )
            vgs[h] = vg

        def prep_v_quant(h):
            vq = vp.tile([P, 2 * D], U32, name="vq", tag="vq", align_bytes=64)
            vs = vp.tile([P, 2 * D], U8, name="vs", tag="vs", align_bytes=64)
            nc.vector.quantize_mx(
                out=vq[:].bitcast(FP8X4), scales=vs[:], in_=vgs[h][:].rearrange("p g d j -> p (g d j)")
            )
            vqs[h] = (vq, vs)

        def stage_qk(n):
            h, i = divmod(n, NI)
            s = []
            for hf in range(2):
                sh = ps_s.tile([P, 512], F32, name="s%d" % hf, tag="s")
                nc.tensor.matmul(
                    sh[:],
                    lhsT=qts[h][:, i * P : (i + 1) * P],
                    rhs=kts[h][:, hf * 512 : (hf + 1) * 512],
                    start=True,
                    stop=True,
                )
                s.append(sh)
            st[n] = {"s": s}

        def stage_max0(n):
            u = up.tile([P, K], F32, name="u", tag="u")
            a0 = small.tile([P, 1], F32, name="a0", tag="a0")
            nc.vector.tensor_scalar(
                out=u[:, 0:512],
                in0=st[n]["s"][0][:],
                scalar1=-SCALE,
                scalar2=None,
                op0=ALU.mult,
                op1=ALU.min,
                accum_out=a0[:],
            )
            st[n]["u"] = u
            st[n]["a0"] = a0

        def stage_max1(n):
            nb = small.tile([P, 1], F32, name="nb", tag="nb")
            if n < FB:
                nc.vector.tensor_scalar(
                    out=st[n]["u"][:, 512:1024],
                    in0=st[n]["s"][1][:],
                    scalar1=-SCALE,
                    scalar2=st[n]["a0"][:, 0:1],
                    op0=ALU.mult,
                    op1=ALU.min,
                    accum_out=nb[:],
                )
                st[n]["nb"] = nb
                return
            a1 = small.tile([P, 1], F32, name="a1", tag="a1")
            nc.vector.tensor_scalar(
                out=st[n]["u"][:, 512:1024],
                in0=st[n]["s"][1][:],
                scalar1=-SCALE,
                scalar2=None,
                op0=ALU.mult,
                op1=ALU.min,
                accum_out=a1[:],
            )
            nc.gpsimd.tensor_scalar(out=nb[:], in0=st[n]["a0"][:], scalar1=a1[:, 0:1], scalar2=None, op0=ALU.min)
            st[n]["nb"] = nb

        def stage_exp(n):
            a = n - first_of[n]
            if a == 0:
                st["acc"] = small.tile([P, size_of[n]], F32, name="acc", tag="acc")
            acc = st["acc"]
            st[n]["acc"] = acc
            e = work.tile([P, K], BF16, name="e", tag="e")
            st[n]["e"] = e
            if n == NT - 1:
                acc = small.tile([P, 2], F32, name="acc2", tag="acc2")
                st[n]["acc"] = acc
                for hf in range(2):
                    nc.scalar.activation(
                        out=e[:, hf * 512 : (hf + 1) * 512],
                        in_=st[n]["u"][:, hf * 512 : (hf + 1) * 512],
                        func=ACT.Exp,
                        bias=st[n]["nb"][:, 0:1],
                        scale=-1.0,
                        accum_out=acc[:, hf : hf + 1],
                    )
                return
            nc.scalar.activation(
                out=e[:],
                in_=st[n]["u"][:],
                func=ACT.Exp,
                bias=st[n]["nb"][:, 0:1],
                scale=-1.0,
                accum_out=acc[:, a : a + 1],
            )

        def stage_tr(n):
            ew = st[n]["e"][:].bitcast(F32)
            if n == NT - 1:
                st[n]["et"] = []
                for g in range(2):
                    et = ps_t.tile([P, 2, P], F32, name="eth", tag="et")
                    for u in range(2):
                        b = 2 * g + u
                        nc.tensor.transpose(et[:, u, :], ew[:, b * P : (b + 1) * P], identf[:])
                    st[n]["et"].append(et)
                return
            et = ps_t.tile([P, 4, P], F32, name="et", tag="et")
            for b in range(4):
                nc.tensor.transpose(et[:, b, :], ew[:, b * P : (b + 1) * P], identf[:])
            st[n]["et"] = et

        def stage_copy(n):
            if n == first_of[n]:
                st["grp"] = gp.tile([P, size_of[n], 2, P, 4], BF16, name="grp", tag="grp", align_bytes=64)
            grp = st["grp"]
            if n == NT - 1:
                st[n]["grp"] = grp
                for g, copy in ((0, nc.vector.tensor_copy), (1, nc.scalar.copy)):
                    copy(
                        out=grp[:, 0, g].rearrange("p t j -> p (t j)").bitcast(F32).rearrange("p (t u) -> p t u", u=2),
                        in_=st[n]["et"][g][:].rearrange("p u t -> p t u"),
                    )
                return
            src = st[n]["et"][:].rearrange("p (g u) t -> p g t u", g=2)
            dst = (
                grp[:, n - first_of[n]]
                .rearrange("p g t j -> p (g t j)")
                .bitcast(F32)
                .rearrange("p (g t u) -> p g t u", g=2, u=2)
            )
            copy = nc.vector.tensor_copy if n == NT - 2 else nc.scalar.copy
            copy(out=dst, in_=src)
            st[n]["grp"] = grp

        def stage_quant(n_last):
            size = size_of[n_last]
            cq = cp.tile([P, size * 2 * P], U32, name="cq", tag="cq", align_bytes=64)
            cs = cp.tile([P, size * 2 * P], U8, name="cs", tag="cs", align_bytes=64)
            if n_last == NT - 1:
                for g in range(2):
                    nc.vector.quantize_mx(
                        out=cq[:, g * P : (g + 1) * P].bitcast(FP8X4),
                        scales=cs[:, g * P : (g + 1) * P],
                        in_=st[n_last]["grp"][:, 0, g].rearrange("p t j -> p (t j)"),
                    )
                acc = small.tile([P, 1], F32, name="acc1", tag="acc1")
                nc.vector.tensor_tensor(
                    out=acc[:], in0=st[n_last]["acc"][:, 0:1], in1=st[n_last]["acc"][:, 1:2], op=ALU.add
                )
                st[n_last]["acc"] = acc
            else:
                nc.vector.quantize_mx(
                    out=cq[:].bitcast(FP8X4),
                    scales=cs[:],
                    in_=st[n_last]["grp"][:].rearrange("p a g t j -> p (a g t j)"),
                )
            for n in range(first_of[n_last], n_last + 1):
                st[n]["cq"] = cq
                st[n]["cs"] = cs
            rin = small.tile([P, size], F32, name="rin", tag="rin")
            nc.vector.reciprocal(out=rin[:], in_=st[n_last]["acc"][:])
            st[n_last]["rin"] = rin

        def stage_pv(n):
            h, i = divmod(n, NI)
            a = n - first_of[n]
            if a == 0:
                if size_of[n] == FB:
                    st["o"] = ps_o.tile([P, FB, D], F32, name="o_ps", tag="o")
                else:
                    st["o"] = ps_s.tile([P, size_of[n], D], F32, name="o_s", tag="s")
            o_ps = st["o"]
            vq, vs = vqs[h]
            for g in range(2):
                c0 = (a * 2 + g) * P
                nc.tensor.matmul_mx(
                    out=o_ps[:, a, :],
                    lhsT=st[n]["cq"][:, c0 : c0 + P].bitcast(FP8X4),
                    lhsT_scale=st[n]["cs"][:, c0 : c0 + P],
                    rhs=vq[:, g * D : (g + 1) * D].bitcast(FP8X4),
                    rhs_scale=vs[:, g * D : (g + 1) * D],
                    start=(g == 0),
                    stop=(g == 1),
                )
            st[n]["o"] = o_ps

        def stage_out(n_last):
            h, i = divmod(n_last, NI)
            size = size_of[n_last]
            osb = work.tile([P, size, D], F32, name="osb", tag="osb")
            nc.vector.tensor_tensor(
                out=osb[:],
                in0=st[n_last]["o"][:],
                in1=st[n_last]["rin"][:].unsqueeze(2).to_broadcast([P, size, D]),
                op=ALU.mult,
            )
            nc.sync.dma_start(out=o_v[:, i - size + 1 : i + 1, h * D : (h + 1) * D], in_=osb[:])

        def step(n):
            if 4 <= n + 3 < NT:
                stage_qk(n + 3)
                stage_max0(n + 3)
            if is_last(n - 4):
                stage_quant(n - 4)
            if is_last(n - 6):
                stage_out(n - 6)
            if 4 <= n + 3 < NT:
                stage_max1(n + 3)
            if is_last(n - 5):
                for m in range(first_of[n - 5], n - 5 + 1):
                    stage_pv(m)
            if 0 <= n < NT:
                stage_exp(n)
            if 0 <= n - 1 < NT:
                stage_tr(n - 1)
            if 0 <= n - 2 < NT:
                stage_copy(n - 2)
            if n == 0:
                prep_v_group(0)
            if n == 2:
                prep_v_quant(0)
            if 0 <= n < NT:
                h = n // NI
                r = n % NI
                if h + 1 < H:
                    if r == 2:
                        copy_k(h + 1)
                    if r == 4:
                        copy_q(h + 1)
                    if r == 0:
                        prep_k(h + 1)
                    if r == 2:
                        prep_q(h + 1)
                    if r == 3:
                        prep_v_group(h + 1)
                    if r == 5:
                        prep_v_quant(h + 1)
                if n % 16 == 1 and n // 16 + 2 < H // 2:
                    load(n // 16 + 2)
                    load_v(n // 16 + 2)

        load(0)
        load(1)
        load_v(0)
        load_v(1)
        with tc.manual_schedule(engines=ORDERED):
            prep_first()
            for n in range(-3, FB):
                step(n)
        for n in range(FB, NT + 7):
            step(n)
